import numpy as np
import ml_dtypes


def mxq(x, axis, fmt="e4m3"):
    dtype, down = {"e4m3": (ml_dtypes.float8_e4m3fn, 7), "e5m2": (ml_dtypes.float8_e5m2, 14)}[fmt]
    v = np.moveaxis(np.asarray(x, np.float32).astype(ml_dtypes.bfloat16).astype(np.float64), axis, -1)
    blocks = v.reshape(v.shape[:-1] + (-1, 32))
    amax = np.abs(blocks).max(-1, keepdims=True)
    byte = np.maximum(np.where(amax > 0, np.frexp(amax)[1] - 1 + 127, 0) - down, 1)
    scale = np.exp2(byte - 127.0)
    codes = (blocks / scale).astype(np.float32).astype(dtype).astype(np.float64)
    return np.moveaxis((codes * scale).reshape(v.shape), -1, axis)


WIDE = False


def mx_kscale(k):
    if not WIDE:
        return np.ones(k)
    levels = np.array([10, -10, 5, -5, 0])
    a = np.random.permutation(np.resize(levels, k // 512 * 4)).reshape(k // 512, 4)
    idx = np.arange(k)
    return np.exp2(a[idx // 512, idx % 128 // 32])


BF16 = ml_dtypes.bfloat16


def bf(x):
    return np.asarray(x, np.float32).astype(BF16)


def f64(x):
    return np.asarray(x).astype(np.float64)


B, C, H, W = 8, 512, 16, 16
HW = H * W
N = B * HW


def setup_inputs():
    t = mx_kscale(C)
    return {"x": bf(np.random.standard_normal((B, C, H, W))),
            "Wq": bf(np.random.standard_normal((C, C)) * 1.5 / np.sqrt(C) * t[:, None]),
            "bq": bf(np.random.standard_normal(C) * 0.3 * t),
            "Wk": bf(np.random.standard_normal((C, C)) * 1.5 / np.sqrt(C) / t[:, None]),
            "bk": bf(np.random.standard_normal(C) * 0.2 / t)}


def reference(x, Wq, bq, Wk, bk):
    x = f64(x)
    scale = 1.0 / np.sqrt(C)
    xq = mxq(x.reshape(B, C, HW), 1, "e4m3")
    q = (xq.transpose(0, 2, 1) @ mxq(f64(Wq), 1, "e4m3").T) + f64(bq)
    q = q.reshape(N, C)
    k = (mxq(f64(Wk), 1, "e4m3") @ xq) + f64(bk)[:, None]
    k = k.transpose(1, 0, 2).reshape(C, N)
    xw = mxq(q, 1, "e4m3") @ mxq(k, 0, "e4m3")
    xw = xw.reshape(N, B, HW).max(-1)
    xw = xw.mean(-1)
    xw = xw.reshape(B, HW) * scale
    e = np.exp(xw - xw.max(-1, keepdims=True))
    xw = e / e.sum(-1, keepdims=True)
    return x * xw.reshape(B, H, W)[:, None]

@@ -1,0 +1,216 @@
+import math
+from contextlib import ExitStack
+
+import concourse.mybir as mybir
+from concourse.masks import make_identity
+
+BF16 = mybir.dt.bfloat16
+F32 = mybir.dt.float32
+U32 = mybir.dt.uint32
+U8 = mybir.dt.uint8
+FP8X4 = mybir.dt.float8_e4m3fn_x4
+ALU = mybir.AluOpType
+ACT = mybir.ActivationFunctionType
+AXIS_X = mybir.AxisListType.X
+
+P = 128
+PACK = 4
+IMAGES = 8
+CHANNELS = P * PACK
+PIXELS = 256
+PAIR = 2 * PIXELS
+PAIRS = IMAGES // 2
+ALL_PIXELS = IMAGES * PIXELS
+CHUNKS = ALL_PIXELS // P
+CHUNKS_PER_PAIR = PAIR // P
+GATE_SCALE = 1.0 / (IMAGES * math.sqrt(CHANNELS))
+
+FLOPS = 2 * 2 * ALL_PIXELS * CHANNELS * CHANNELS + 2 * ALL_PIXELS * ALL_PIXELS * CHANNELS
+
+
+def tile_coattlayer_pa_kernel(tc, x, Wq, bq, Wk, bk, out):
+    nc = tc.nc
+    with ExitStack() as stack:
+        keep = stack.enter_context(tc.tile_pool(name="keep", bufs=1))
+        stage = stack.enter_context(tc.tile_pool(name="stage", bufs=2))
+        small = stack.enter_context(tc.tile_pool(name="small", bufs=2))
+        results = stack.enter_context(tc.tile_pool(name="results", bufs=3))
+        psum_proj = stack.enter_context(tc.psum_pool(name="psum_proj", bufs=3))
+        psum_score = stack.enter_context(tc.psum_pool(name="psum_score", bufs=4))
+        psum_spread = stack.enter_context(tc.psum_pool(name="psum_spread", bufs=1))
+
+        x_view = x.rearrange("b (p j) h w -> p b j (h w)", j=PACK)
+        out_view = out.rearrange("b (p j) h w -> b p j (h w)", j=PACK)
+        x_sb = keep.tile([P, IMAGES, PACK, PIXELS], BF16)
+        wk_rows = keep.tile([P, PACK * CHANNELS], BF16)
+        wq_rows = keep.tile([P, PACK * CHANNELS], BF16)
+        nc.sync.dma_start(out=wk_rows[:], in_=Wk.rearrange("(p t) c -> p (t c)", t=PACK))
+        nc.sync.dma_start(out=x_sb[:, 0:2], in_=x_view[:, 0:2])
+        nc.sync.dma_start(out=wq_rows[:], in_=Wq.rearrange("(p t) c -> p (t c)", t=PACK))
+        for pair in range(1, PAIRS):
+            nc.sync.dma_start(out=x_sb[:, 2 * pair : 2 * pair + 2], in_=x_view[:, 2 * pair : 2 * pair + 2])
+        bk_raw = keep.tile([P, PACK], BF16)
+        bq_raw = keep.tile([P, PACK], BF16)
+        nc.scalar.dma_start(out=bk_raw[:], in_=bk.rearrange("(p t) -> p t", t=PACK))
+        nc.scalar.dma_start(out=bq_raw[:], in_=bq.rearrange("(p t) -> p t", t=PACK))
+
+        ident = keep.tile([P, P], F32)
+        make_identity(nc, ident[:])
+        bk_f32 = keep.tile([P, PACK], F32)
+        bq_f32 = keep.tile([P, PACK], F32)
+        nc.vector.tensor_copy(out=bk_f32[:], in_=bk_raw[:])
+        nc.vector.tensor_copy(out=bq_f32[:], in_=bq_raw[:])
+
+        x_codes = keep.tile([P, ALL_PIXELS], U32, align_bytes=64)
+        x_scales = keep.tile([P, ALL_PIXELS], U8, align_bytes=64)
+        wk_codes = keep.tile([P, CHANNELS], U32, align_bytes=64)
+        wk_scales = keep.tile([P, CHANNELS], U8, align_bytes=64)
+        wq_codes = keep.tile([P, CHANNELS], U32, align_bytes=64)
+        wq_scales = keep.tile([P, CHANNELS], U8, align_bytes=64)
+        k_codes = keep.tile([P, ALL_PIXELS], U32, align_bytes=64)
+        k_scales = keep.tile([P, ALL_PIXELS], U8, align_bytes=64)
+        q_codes = keep.tile([P, ALL_PIXELS], U32, align_bytes=64)
+        q_scales = keep.tile([P, ALL_PIXELS], U8, align_bytes=64)
+        best = keep.tile([P, CHUNKS, IMAGES], F32)
+
+        def quantise_weight(rows, codes, scales):
+            words = rows[:].bitcast(F32).rearrange("p (t q u) -> p t u q", t=PACK, u=2)
+            grouped = stage.tile([P, PACK * CHANNELS], BF16, tag="w_grouped", align_bytes=64)
+            grouped_words = grouped[:].bitcast(F32).rearrange("p (t d u) -> p t d u", t=PACK, u=2)
+            for half in range(2):
+                turned = psum_score.tile([P, 2, 2, P], F32, tag="score")
+                for a in range(2):
+                    for u in range(2):
+                        nc.tensor.transpose(
+                            out=turned[:, a, u, :], in_=words[:, 2 * half + a, u, :], identity=ident[:]
+                        )
+                nc.scalar.copy(
+                    out=grouped_words[:, 2 * half : 2 * half + 2],
+                    in_=turned[:].rearrange("p a u d -> p a d u"),
+                )
+            nc.vector.quantize_mx(out=codes[:].bitcast(FP8X4), scales=scales[:], in_=grouped[:])
+
+        def quantise_x(pair):
+            grouped = stage.tile([P, 2, PIXELS, PACK], BF16, tag="x_grouped", bufs=PAIRS, align_bytes=64)
+            for i in range(2):
+                nc.vector.tensor_copy(
+                    out=grouped[:, i].rearrange("p (c r) j -> p c j r", r=4),
+                    in_=x_sb[:, 2 * pair + i].rearrange("p j (c r) -> p c j r", r=4),
+                )
+            cols = slice(pair * PAIR, (pair + 1) * PAIR)
+            nc.vector.quantize_mx(
+                out=x_codes[:, cols].bitcast(FP8X4),
+                scales=x_scales[:, cols],
+                in_=grouped[:].rearrange("p i w j -> p (i w j)"),
+            )
+
+        def project(w_codes, w_scales, bias, codes, scales, pair):
+            cols = slice(pair * PAIR, (pair + 1) * PAIR)
+            planes = stage.tile([P, PACK, PAIR], BF16, tag="planes")
+            for t in range(PACK):
+                acc = psum_proj.tile([P, PAIR], F32, tag="proj")
+                nc.tensor.matmul_mx(
+                    out=acc[:],
+                    lhsT=w_codes[:, t * P : (t + 1) * P].bitcast(FP8X4),
+                    lhsT_scale=w_scales[:, t * P : (t + 1) * P],
+                    rhs=x_codes[:, cols].bitcast(FP8X4),
+                    rhs_scale=x_scales[:, cols],
+                    start=True,
+                    stop=True,
+                )
+                nc.scalar.activation(
+                    out=planes[:, t, :], in_=acc[:], func=ACT.Identity, bias=bias[:, t : t + 1], scale=1.0
+                )
+            grouped = stage.tile([P, PAIR, PACK], BF16, tag="grouped", align_bytes=64)
+            for i in range(2):
+                pix = slice(i * PIXELS, (i + 1) * PIXELS)
+                nc.gpsimd.tensor_scalar(
+                    out=grouped[:, pix, :],
+                    in0=planes[:, :, pix].rearrange("p t n -> p n t"),
+                    scalar1=1.0,
+                    scalar2=0.0,
+                    op0=ALU.mult,
+                    op1=ALU.add,
+                )
+            nc.vector.quantize_mx(
+                out=codes[:, cols].bitcast(FP8X4),
+                scales=scales[:, cols],
+                in_=grouped[:].rearrange("p n t -> p (n t)"),
+            )
+
+        def score(chunk, pair):
+            cols = slice(pair * PAIR, (pair + 1) * PAIR)
+            acc = psum_score.tile([P, PAIR], F32, tag="score")
+            nc.tensor.matmul_mx(
+                out=acc[:],
+                lhsT=q_codes[:, chunk * P : (chunk + 1) * P].bitcast(FP8X4),
+                lhsT_scale=q_scales[:, chunk * P : (chunk + 1) * P],
+                rhs=k_codes[:, cols].bitcast(FP8X4),
+                rhs_scale=k_scales[:, cols],
+                start=True,
+                stop=True,
+            )
+            nc.vector.tensor_reduce(
+                out=best[:, chunk, 2 * pair : 2 * pair + 2],
+                in_=acc[:].rearrange("p (i m) -> p i m", i=2),
+                axis=AXIS_X,
+                op=ALU.max,
+            )
+
+        def finish(image):
+            total = small.tile([P, 2], F32, tag="total")
+            nc.vector.tensor_reduce(
+                out=total[:], in_=best[:, 2 * image : 2 * image + 2, :], axis=AXIS_X, op=ALU.add
+            )
+            spread = psum_spread.tile([P, PIXELS], F32, tag="spread")
+            for h in range(2):
+                nc.tensor.transpose(
+                    out=spread[:, h * P : (h + 1) * P],
+                    in_=total[:, h : h + 1].to_broadcast([P, P]),
+                    identity=ident[:],
+                )
+            top = small.tile([P, 1], F32, tag="top")
+            nc.vector.tensor_reduce(out=top[:], in_=spread[:], axis=AXIS_X, op=ALU.max)
+            shift = small.tile([P, 1], F32, tag="shift")
+            nc.scalar.mul(out=shift[:], in_=top[:], mul=-GATE_SCALE)
+            numer = small.tile([P, PIXELS], F32, tag="numer")
+            denom = small.tile([P, 1], F32, tag="denom")
+            nc.scalar.activation(
+                out=numer[:], in_=spread[:], func=ACT.Exp, bias=shift[:, 0:1], scale=GATE_SCALE, accum_out=denom[:]
+            )
+            inverse = small.tile([P, 1], F32, tag="inverse")
+            nc.vector.reciprocal(out=inverse[:], in_=denom[:])
+            gate = small.tile([P, PIXELS], F32, tag="gate")
+            nc.scalar.activation(out=gate[:], in_=numer[:], func=ACT.Copy, scale=inverse[:, 0:1])
+            product = results.tile([P, PACK, PIXELS], F32, tag="product")
+            nc.gpsimd.tensor_tensor(
+                out=product[:],
+                in0=x_sb[:, image],
+                in1=gate[:].unsqueeze(1).to_broadcast([P, PACK, PIXELS]),
+                op=ALU.mult,
+            )
+            nc.sync.dma_start(out=out_view[image], in_=product[:])
+
+        quantise_weight(wk_rows, wk_codes, wk_scales)
+        quantise_x(0)
+        quantise_weight(wq_rows, wq_codes, wq_scales)
+        for pair in range(1, PAIRS):
+            quantise_x(pair)
+
+        project(wk_codes, wk_scales, bk_f32, k_codes, k_scales, 0)
+        project(wq_codes, wq_scales, bq_f32, q_codes, q_scales, 0)
+        for pair in range(1, PAIRS):
+            project(wk_codes, wk_scales, bk_f32, k_codes, k_scales, pair)
+        for pair in range(1, PAIRS):
+            project(wq_codes, wq_scales, bq_f32, q_codes, q_scales, pair)
+
+        for pair in range(PAIRS):
+            for chunk in range(CHUNKS_PER_PAIR):
+                score(chunk, pair)
+        finish(0)
+        finish(1)
+        for chunk in range(CHUNKS_PER_PAIR, CHUNKS):
+            for pair in range(PAIRS):
+                score(chunk, pair)
+            if chunk % 2 == 1:
+                finish(chunk // 2)

@@ -25,6 +25,8 @@ CHUNKS = ALL_PIXELS // P
 CHUNKS_PER_PAIR = PAIR // P
 GATE_SCALE = 1.0 / (IMAGES * math.sqrt(CHANNELS))
 
+LEAD = 2
+
 FLOPS = 2 * 2 * ALL_PIXELS * CHANNELS * CHANNELS + 2 * ALL_PIXELS * ALL_PIXELS * CHANNELS
 
 
@@ -33,19 +35,20 @@ def tile_coattlayer_pa_kernel(tc, x, Wq, bq, Wk, bk, out):
     with ExitStack() as stack:
         keep = stack.enter_context(tc.tile_pool(name="keep", bufs=1))
         stage = stack.enter_context(tc.tile_pool(name="stage", bufs=2))
-        small = stack.enter_context(tc.tile_pool(name="small", bufs=2))
+        small = stack.enter_context(tc.tile_pool(name="small", bufs=3))
         results = stack.enter_context(tc.tile_pool(name="results", bufs=3))
         psum_proj = stack.enter_context(tc.psum_pool(name="psum_proj", bufs=3))
         psum_score = stack.enter_context(tc.psum_pool(name="psum_score", bufs=4))
         psum_spread = stack.enter_context(tc.psum_pool(name="psum_spread", bufs=1))
+        stack.enter_context(tc.manual_schedule())
 
         x_view = x.rearrange("b (p j) h w -> p b j (h w)", j=PACK)
         out_view = out.rearrange("b (p j) h w -> b p j (h w)", j=PACK)
         x_sb = keep.tile([P, IMAGES, PACK, PIXELS], BF16)
         wk_rows = keep.tile([P, PACK * CHANNELS], BF16)
         wq_rows = keep.tile([P, PACK * CHANNELS], BF16)
-        nc.sync.dma_start(out=wk_rows[:], in_=Wk.rearrange("(p t) c -> p (t c)", t=PACK))
         nc.sync.dma_start(out=x_sb[:, 0:2], in_=x_view[:, 0:2])
+        nc.sync.dma_start(out=wk_rows[:], in_=Wk.rearrange("(p t) c -> p (t c)", t=PACK))
         nc.sync.dma_start(out=wq_rows[:], in_=Wq.rearrange("(p t) c -> p (t c)", t=PACK))
         for pair in range(1, PAIRS):
             nc.sync.dma_start(out=x_sb[:, 2 * pair : 2 * pair + 2], in_=x_view[:, 2 * pair : 2 * pair + 2])
@@ -58,8 +61,8 @@ def tile_coattlayer_pa_kernel(tc, x, Wq, bq, Wk, bk, out):
         make_identity(nc, ident[:])
         bk_f32 = keep.tile([P, PACK], F32)
         bq_f32 = keep.tile([P, PACK], F32)
-        nc.vector.tensor_copy(out=bk_f32[:], in_=bk_raw[:])
-        nc.vector.tensor_copy(out=bq_f32[:], in_=bq_raw[:])
+        nc.gpsimd.tensor_copy(out=bk_f32[:], in_=bk_raw[:])
+        nc.gpsimd.tensor_copy(out=bq_f32[:], in_=bq_raw[:])
 
         x_codes = keep.tile([P, ALL_PIXELS], U32, align_bytes=64)
         x_scales = keep.tile([P, ALL_PIXELS], U8, align_bytes=64)
@@ -72,8 +75,13 @@ def tile_coattlayer_pa_kernel(tc, x, Wq, bq, Wk, bk, out):
         q_codes = keep.tile([P, ALL_PIXELS], U32, align_bytes=64)
         q_scales = keep.tile([P, ALL_PIXELS], U8, align_bytes=64)
         best = keep.tile([P, CHUNKS, IMAGES], F32)
+        side_k = {"w_codes": wk_codes, "w_scales": wk_scales, "bias": bk_f32, "codes": k_codes, "scales": k_scales}
+        side_q = {"w_codes": wq_codes, "w_scales": wq_scales, "bias": bq_f32, "codes": q_codes, "scales": q_scales}
 
-        def quantise_weight(rows, codes, scales):
+        def pair_cols(pair):
+            return slice(pair * PAIR, (pair + 1) * PAIR)
+
+        def turn_weight(rows):
             words = rows[:].bitcast(F32).rearrange("p (t q u) -> p t u q", t=PACK, u=2)
             grouped = stage.tile([P, PACK * CHANNELS], BF16, tag="w_grouped", align_bytes=64)
             grouped_words = grouped[:].bitcast(F32).rearrange("p (t d u) -> p t d u", t=PACK, u=2)
@@ -88,40 +96,59 @@ def tile_coattlayer_pa_kernel(tc, x, Wq, bq, Wk, bk, out):
                     out=grouped_words[:, 2 * half : 2 * half + 2],
                     in_=turned[:].rearrange("p a u d -> p a d u"),
                 )
-            nc.vector.quantize_mx(out=codes[:].bitcast(FP8X4), scales=scales[:], in_=grouped[:])
+            return grouped
 
-        def quantise_x(pair):
+        def regroup_x(pair):
             grouped = stage.tile([P, 2, PIXELS, PACK], BF16, tag="x_grouped", bufs=PAIRS, align_bytes=64)
             for i in range(2):
                 nc.vector.tensor_copy(
                     out=grouped[:, i].rearrange("p (c r) j -> p c j r", r=4),
                     in_=x_sb[:, 2 * pair + i].rearrange("p j (c r) -> p c j r", r=4),
                 )
-            cols = slice(pair * PAIR, (pair + 1) * PAIR)
+            return grouped
+
+        def quantise_x(pair, grouped):
             nc.vector.quantize_mx(
-                out=x_codes[:, cols].bitcast(FP8X4),
-                scales=x_scales[:, cols],
+                out=x_codes[:, pair_cols(pair)].bitcast(FP8X4),
+                scales=x_scales[:, pair_cols(pair)],
                 in_=grouped[:].rearrange("p i w j -> p (i w j)"),
             )
 
-        def project(w_codes, w_scales, bias, codes, scales, pair):
-            cols = slice(pair * PAIR, (pair + 1) * PAIR)
-            planes = stage.tile([P, PACK, PAIR], BF16, tag="planes")
+        def project_pass(side, pair, planes, t):
+            acc = psum_proj.tile([P, PAIR], F32, tag="proj")
+            nc.tensor.matmul_mx(
+                out=acc[:],
+                lhsT=side["w_codes"][:, t * P : (t + 1) * P].bitcast(FP8X4),
+                lhsT_scale=side["w_scales"][:, t * P : (t + 1) * P],
+                rhs=x_codes[:, pair_cols(pair)].bitcast(FP8X4),
+                rhs_scale=x_scales[:, pair_cols(pair)],
+                start=True,
+                stop=True,
+            )
+            nc.scalar.activation(
+                out=planes[:, t, :], in_=acc[:], func=ACT.Identity, bias=side["bias"][:, t : t + 1], scale=1.0
+            )
+
+        def new_planes():
+            planes = stage.tile([P, PACK, PAIR], BF16, tag="planes", bufs=3)
+            return planes
+
+        def project(side, pair):
+            planes = new_planes()
             for t in range(PACK):
-                acc = psum_proj.tile([P, PAIR], F32, tag="proj")
-                nc.tensor.matmul_mx(
-                    out=acc[:],
-                    lhsT=w_codes[:, t * P : (t + 1) * P].bitcast(FP8X4),
-                    lhsT_scale=w_scales[:, t * P : (t + 1) * P],
-                    rhs=x_codes[:, cols].bitcast(FP8X4),
-                    rhs_scale=x_scales[:, cols],
-                    start=True,
-                    stop=True,
-                )
-                nc.scalar.activation(
-                    out=planes[:, t, :], in_=acc[:], func=ACT.Identity, bias=bias[:, t : t + 1], scale=1.0
-                )
-            grouped = stage.tile([P, PAIR, PACK], BF16, tag="grouped", align_bytes=64)
+                project_pass(side, pair, planes, t)
+            return planes
+
+        def regroup_on_vector(planes):
+            grouped = stage.tile([P, PAIR, PACK], BF16, tag="grouped", bufs=4, align_bytes=64)
+            nc.vector.tensor_copy(
+                out=grouped[:].rearrange("p (c r) t -> p c t r", r=4),
+                in_=planes[:].rearrange("p t (c r) -> p c t r", r=4),
+            )
+            return grouped
+
+        def regroup_on_gpsimd(planes):
+            grouped = stage.tile([P, PAIR, PACK], BF16, tag="grouped", bufs=4, align_bytes=64)
             for i in range(2):
                 pix = slice(i * PIXELS, (i + 1) * PIXELS)
                 nc.gpsimd.tensor_scalar(
@@ -132,56 +159,89 @@ def tile_coattlayer_pa_kernel(tc, x, Wq, bq, Wk, bk, out):
                     op0=ALU.mult,
                     op1=ALU.add,
                 )
+            return grouped
+
+        def quantise(side, pair, grouped):
             nc.vector.quantize_mx(
-                out=codes[:, cols].bitcast(FP8X4),
-                scales=scales[:, cols],
+                out=side["codes"][:, pair_cols(pair)].bitcast(FP8X4),
+                scales=side["scales"][:, pair_cols(pair)],
                 in_=grouped[:].rearrange("p n t -> p (n t)"),
             )
 
-        def score(chunk, pair):
-            cols = slice(pair * PAIR, (pair + 1) * PAIR)
+        units = [(chunk, pair) for pair in range(PAIRS) for chunk in range(CHUNKS_PER_PAIR)]
+        units += [(chunk, pair) for chunk in range(CHUNKS_PER_PAIR, CHUNKS) for pair in range(PAIRS)]
+        banks = {}
+
+        def score_pass(n):
+            if n >= len(units):
+                return
+            chunk, pair = units[n]
             acc = psum_score.tile([P, PAIR], F32, tag="score")
             nc.tensor.matmul_mx(
                 out=acc[:],
                 lhsT=q_codes[:, chunk * P : (chunk + 1) * P].bitcast(FP8X4),
                 lhsT_scale=q_scales[:, chunk * P : (chunk + 1) * P],
-                rhs=k_codes[:, cols].bitcast(FP8X4),
-                rhs_scale=k_scales[:, cols],
+                rhs=k_codes[:, pair_cols(pair)].bitcast(FP8X4),
+                rhs_scale=k_scales[:, pair_cols(pair)],
                 start=True,
                 stop=True,
             )
+            banks[n] = acc
+
+        def take_maxima(n):
+            chunk, pair = units[n]
             nc.vector.tensor_reduce(
                 out=best[:, chunk, 2 * pair : 2 * pair + 2],
-                in_=acc[:].rearrange("p (i m) -> p i m", i=2),
+                in_=banks[n][:].rearrange("p (i m) -> p i m", i=2),
                 axis=AXIS_X,
                 op=ALU.max,
             )
 
-        def finish(image):
+        totals = {}
+        spreads = {}
+        numers = {}
+        denoms = {}
+
+        def add_up(image):
             total = small.tile([P, 2], F32, tag="total")
             nc.vector.tensor_reduce(
                 out=total[:], in_=best[:, 2 * image : 2 * image + 2, :], axis=AXIS_X, op=ALU.add
             )
+            totals[image] = total
+
+        def spread_out(image):
             spread = psum_spread.tile([P, PIXELS], F32, tag="spread")
             for h in range(2):
                 nc.tensor.transpose(
                     out=spread[:, h * P : (h + 1) * P],
-                    in_=total[:, h : h + 1].to_broadcast([P, P]),
+                    in_=totals[image][:, h : h + 1].to_broadcast([P, P]),
                     identity=ident[:],
                 )
+            spreads[image] = spread
+
+        def exponentials(image):
             top = small.tile([P, 1], F32, tag="top")
-            nc.vector.tensor_reduce(out=top[:], in_=spread[:], axis=AXIS_X, op=ALU.max)
+            nc.vector.tensor_reduce(out=top[:], in_=spreads[image][:], axis=AXIS_X, op=ALU.max)
             shift = small.tile([P, 1], F32, tag="shift")
             nc.scalar.mul(out=shift[:], in_=top[:], mul=-GATE_SCALE)
             numer = small.tile([P, PIXELS], F32, tag="numer")
             denom = small.tile([P, 1], F32, tag="denom")
             nc.scalar.activation(
-                out=numer[:], in_=spread[:], func=ACT.Exp, bias=shift[:, 0:1], scale=GATE_SCALE, accum_out=denom[:]
+                out=numer[:],
+                in_=spreads[image][:],
+                func=ACT.Exp,
+                bias=shift[:, 0:1],
+                scale=GATE_SCALE,
+                accum_out=denom[:],
             )
+            numers[image] = numer
+            denoms[image] = denom
+
+        def gate_and_store(image):
             inverse = small.tile([P, 1], F32, tag="inverse")
-            nc.vector.reciprocal(out=inverse[:], in_=denom[:])
+            nc.vector.reciprocal(out=inverse[:], in_=denoms[image][:])
             gate = small.tile([P, PIXELS], F32, tag="gate")
-            nc.scalar.activation(out=gate[:], in_=numer[:], func=ACT.Copy, scale=inverse[:, 0:1])
+            nc.scalar.activation(out=gate[:], in_=numers[image][:], func=ACT.Copy, scale=inverse[:, 0:1])
             product = results.tile([P, PACK, PIXELS], F32, tag="product")
             nc.gpsimd.tensor_tensor(
                 out=product[:],
@@ -191,26 +251,84 @@ def tile_coattlayer_pa_kernel(tc, x, Wq, bq, Wk, bk, out):
             )
             nc.sync.dma_start(out=out_view[image], in_=product[:])
 
-        quantise_weight(wk_rows, wk_codes, wk_scales)
-        quantise_x(0)
-        quantise_weight(wq_rows, wq_codes, wq_scales)
-        for pair in range(1, PAIRS):
-            quantise_x(pair)
+        def gate_and_store_on_vector(image):
+            inverse = small.tile([P, 1], F32, tag="inverse")
+            nc.vector.reciprocal(out=inverse[:], in_=denoms[image][:])
+            product = results.tile([P, PACK, PIXELS], F32, tag="product")
+            for half in range(2):
+                rows = slice(2 * half, 2 * half + 2)
+                nc.vector.scalar_tensor_tensor(
+                    out=product[:, rows, :],
+                    in0=x_sb[:, image, rows, :],
+                    scalar=inverse[:, 0:1],
+                    in1=numers[image][:].unsqueeze(1).to_broadcast([P, 2, PIXELS]),
+                    op0=ALU.mult,
+                    op1=ALU.mult,
+                )
+                nc.sync.dma_start(out=out_view[image][:, rows, :], in_=product[:, rows, :])
 
-        project(wk_codes, wk_scales, bk_f32, k_codes, k_scales, 0)
-        project(wq_codes, wq_scales, bq_f32, q_codes, q_scales, 0)
-        for pair in range(1, PAIRS):
-            project(wk_codes, wk_scales, bk_f32, k_codes, k_scales, pair)
-        for pair in range(1, PAIRS):
-            project(wq_codes, wq_scales, bq_f32, q_codes, q_scales, pair)
+        x_grouped = regroup_x(0)
+        quantise_x(0, x_grouped)
+        wk_grouped = turn_weight(wk_rows)
+        wq_grouped = turn_weight(wq_rows)
+        nc.vector.quantize_mx(out=wk_codes[:].bitcast(FP8X4), scales=wk_scales[:], in_=wk_grouped[:])
+        k0_planes = project(side_k, 0)
+        x_grouped = regroup_x(1)
+        nc.vector.quantize_mx(out=wq_codes[:].bitcast(FP8X4), scales=wq_scales[:], in_=wq_grouped[:])
+        q0_planes = project(side_q, 0)
+        quantise_x(1, x_grouped)
+        k1_planes = project(side_k, 1)
+        x_grouped = regroup_x(2)
+        k0_grouped = regroup_on_vector(k0_planes)
+        quantise_x(2, x_grouped)
+        k2_planes = project(side_k, 2)
+        waiting = {("k", 2): regroup_on_gpsimd(k2_planes)}
+        quantise(side_k, 0, k0_grouped)
+        q0_grouped = regroup_on_vector(q0_planes)
+        x_grouped = regroup_x(3)
+        quantise(side_q, 0, q0_grouped)
+        for n in range(LEAD):
+            score_pass(n)
+        quantise_x(3, x_grouped)
 
-        for pair in range(PAIRS):
+        sides = {"k": side_k, "q": side_q}
+        carried = (("k", 3), ("q", 1), ("q", 2), ("q", 3))
+        for block in range(PAIRS):
+            name, pair = carried[block]
+            planes = new_planes()
             for chunk in range(CHUNKS_PER_PAIR):
-                score(chunk, pair)
-        finish(0)
-        finish(1)
-        for chunk in range(CHUNKS_PER_PAIR, CHUNKS):
-            for pair in range(PAIRS):
-                score(chunk, pair)
-            if chunk % 2 == 1:
-                finish(chunk // 2)
+                n = block * CHUNKS_PER_PAIR + chunk
+                project_pass(sides[name], pair, planes, chunk)
+                if block == 0 and chunk == 0:
+                    waiting[("k", 1)] = regroup_on_vector(k1_planes)
+                if chunk == LEAD:
+                    due = ("k", block + 1) if block + 1 < PAIRS else ("q", 1)
+                    quantise(sides[due[0]], due[1], waiting[due])
+                score_pass(n + LEAD)
+                take_maxima(n)
+            waiting[(name, pair)] = regroup_on_gpsimd(planes)
+        add_up(0)
+        add_up(1)
+
+        for image in range(2, IMAGES):
+            riders = (0, 1) if image == 2 else (image - 1, None)
+            for half in range(2):
+                chunk = 2 * image + half
+                rider = riders[half]
+                for pair in range(PAIRS):
+                    n = chunk * PAIRS + pair
+                    if (n + LEAD) % (CHUNKS_PER_PAIR * PAIRS) == 0 and n + LEAD < len(units):
+                        due = ("q", (n + LEAD) // (CHUNKS_PER_PAIR * PAIRS))
+                        quantise(side_q, due[1], waiting[due])
+                    score_pass(n + LEAD)
+                    take_maxima(n)
+                    if rider is not None and pair == 0:
+                        spread_out(rider)
+                    if rider is not None and pair == 1:
+                        exponentials(rider)
+                    if rider is not None and pair == 3:
+                        gate_and_store(rider)
+            add_up(image)
+        spread_out(IMAGES - 1)
+        exponentials(IMAGES - 1)
+        gate_and_store_on_vector(IMAGES - 1)

@@ -26,6 +26,9 @@ CHUNKS_PER_PAIR = PAIR // P
 GATE_SCALE = 1.0 / (IMAGES * math.sqrt(CHANNELS))
 
 LEAD = 2
+SPREAD_LAG = 2
+EXP_LAG = 4
+GATE_LAG = 7
 
 FLOPS = 2 * 2 * ALL_PIXELS * CHANNELS * CHANNELS + 2 * ALL_PIXELS * ALL_PIXELS * CHANNELS
 
@@ -37,9 +40,8 @@ def tile_coattlayer_pa_kernel(tc, x, Wq, bq, Wk, bk, out):
         stage = stack.enter_context(tc.tile_pool(name="stage", bufs=2))
         small = stack.enter_context(tc.tile_pool(name="small", bufs=3))
         results = stack.enter_context(tc.tile_pool(name="results", bufs=3))
-        psum_proj = stack.enter_context(tc.psum_pool(name="psum_proj", bufs=3))
+        psum_proj = stack.enter_context(tc.psum_pool(name="psum_proj", bufs=4))
         psum_score = stack.enter_context(tc.psum_pool(name="psum_score", bufs=4))
-        psum_spread = stack.enter_context(tc.psum_pool(name="psum_spread", bufs=1))
         stack.enter_context(tc.manual_schedule())
 
         x_view = x.rearrange("b (p j) h w -> p b j (h w)", j=PACK)
@@ -210,7 +212,7 @@ def tile_coattlayer_pa_kernel(tc, x, Wq, bq, Wk, bk, out):
             totals[image] = total
 
         def spread_out(image):
-            spread = psum_spread.tile([P, PIXELS], F32, tag="spread")
+            spread = psum_proj.tile([P, PIXELS], F32, tag="proj")
             for h in range(2):
                 nc.tensor.transpose(
                     out=spread[:, h * P : (h + 1) * P],
@@ -240,32 +242,41 @@ def tile_coattlayer_pa_kernel(tc, x, Wq, bq, Wk, bk, out):
         def gate_and_store(image):
             inverse = small.tile([P, 1], F32, tag="inverse")
             nc.vector.reciprocal(out=inverse[:], in_=denoms[image][:])
-            gate = small.tile([P, PIXELS], F32, tag="gate")
-            nc.scalar.activation(out=gate[:], in_=numers[image][:], func=ACT.Copy, scale=inverse[:, 0:1])
             product = results.tile([P, PACK, PIXELS], F32, tag="product")
-            nc.gpsimd.tensor_tensor(
-                out=product[:],
-                in0=x_sb[:, image],
-                in1=gate[:].unsqueeze(1).to_broadcast([P, PACK, PIXELS]),
-                op=ALU.mult,
-            )
-            nc.sync.dma_start(out=out_view[image], in_=product[:])
-
-        def gate_and_store_on_vector(image):
-            inverse = small.tile([P, 1], F32, tag="inverse")
-            nc.vector.reciprocal(out=inverse[:], in_=denoms[image][:])
-            product = results.tile([P, PACK, PIXELS], F32, tag="product")
-            for half in range(2):
-                rows = slice(2 * half, 2 * half + 2)
-                nc.vector.scalar_tensor_tensor(
-                    out=product[:, rows, :],
-                    in0=x_sb[:, image, rows, :],
-                    scalar=inverse[:, 0:1],
-                    in1=numers[image][:].unsqueeze(1).to_broadcast([P, 2, PIXELS]),
-                    op0=ALU.mult,
-                    op1=ALU.mult,
+            if image < IMAGES - 1:
+                gate = small.tile([P, PIXELS], F32, tag="gate")
+                nc.scalar.activation(out=gate[:], in_=numers[image][:], func=ACT.Copy, scale=inverse[:, 0:1])
+                nc.gpsimd.tensor_tensor(
+                    out=product[:],
+                    in0=x_sb[:, image],
+                    in1=gate[:].unsqueeze(1).to_broadcast([P, PACK, PIXELS]),
+                    op=ALU.mult,
                 )
-                nc.sync.dma_start(out=out_view[image][:, rows, :], in_=product[:, rows, :])
+                nc.sync.dma_start(out=out_view[image], in_=product[:])
+            else:
+                for half in range(2):
+                    rows = slice(2 * half, 2 * half + 2)
+                    nc.vector.scalar_tensor_tensor(
+                        out=product[:, rows, :],
+                        in0=x_sb[:, image, rows, :],
+                        scalar=inverse[:, 0:1],
+                        in1=numers[image][:].unsqueeze(1).to_broadcast([P, 2, PIXELS]),
+                        op0=ALU.mult,
+                        op1=ALU.mult,
+                    )
+                    nc.sync.dma_start(out=out_view[image][:, rows, :], in_=product[:, rows, :])
+
+        def endings(n):
+            for image in range(IMAGES):
+                last_unit = max(CHUNKS_PER_PAIR, 2 * image + 2) * PAIRS - 1
+                if n == last_unit:
+                    add_up(image)
+                if n == last_unit + SPREAD_LAG:
+                    spread_out(image)
+                if n == last_unit + EXP_LAG:
+                    exponentials(image)
+                if n == last_unit + GATE_LAG:
+                    gate_and_store(image)
 
         x_grouped = regroup_x(0)
         quantise_x(0, x_grouped)
@@ -306,29 +317,14 @@ def tile_coattlayer_pa_kernel(tc, x, Wq, bq, Wk, bk, out):
                     quantise(sides[due[0]], due[1], waiting[due])
                 score_pass(n + LEAD)
                 take_maxima(n)
+                endings(n)
             waiting[(name, pair)] = regroup_on_gpsimd(planes)
-        add_up(0)
-        add_up(1)
 
-        for image in range(2, IMAGES):
-            riders = (0, 1) if image == 2 else (image - 1, None)
-            for half in range(2):
-                chunk = 2 * image + half
-                rider = riders[half]
-                for pair in range(PAIRS):
-                    n = chunk * PAIRS + pair
-                    if (n + LEAD) % (CHUNKS_PER_PAIR * PAIRS) == 0 and n + LEAD < len(units):
-                        due = ("q", (n + LEAD) // (CHUNKS_PER_PAIR * PAIRS))
-                        quantise(side_q, due[1], waiting[due])
-                    score_pass(n + LEAD)
-                    take_maxima(n)
-                    if rider is not None and pair == 0:
-                        spread_out(rider)
-                    if rider is not None and pair == 1:
-                        exponentials(rider)
-                    if rider is not None and pair == 3:
-                        gate_and_store(rider)
-            add_up(image)
-        spread_out(IMAGES - 1)
-        exponentials(IMAGES - 1)
-        gate_and_store_on_vector(IMAGES - 1)
+        for n in range(CHUNKS_PER_PAIR * PAIRS, len(units) + GATE_LAG + 1):
+            if (n + LEAD) % (CHUNKS_PER_PAIR * PAIRS) == 0 and n + LEAD < len(units):
+                due = ("q", (n + LEAD) // (CHUNKS_PER_PAIR * PAIRS))
+                quantise(side_q, due[1], waiting[due])
+            score_pass(n + LEAD)
+            if n < len(units):
+                take_maxima(n)
+            endings(n)

@@ -25,8 +25,9 @@ CHUNKS = ALL_PIXELS // P
 CHUNKS_PER_PAIR = PAIR // P
 GATE_SCALE = 1.0 / (IMAGES * math.sqrt(CHANNELS))
 
-LEAD = 2
-SPREAD_LAG = 2
+EARLY_CHUNKS = 2 * CHUNKS_PER_PAIR
+LEAD = 3
+SPREAD_LAG = 1
 EXP_LAG = 4
 GATE_LAG = 7
 
@@ -38,8 +39,8 @@ def tile_coattlayer_pa_kernel(tc, x, Wq, bq, Wk, bk, out):
     with ExitStack() as stack:
         keep = stack.enter_context(tc.tile_pool(name="keep", bufs=1))
         stage = stack.enter_context(tc.tile_pool(name="stage", bufs=2))
-        small = stack.enter_context(tc.tile_pool(name="small", bufs=3))
-        results = stack.enter_context(tc.tile_pool(name="results", bufs=3))
+        small = stack.enter_context(tc.tile_pool(name="small", bufs=4))
+        results = stack.enter_context(tc.tile_pool(name="results", bufs=4))
         psum_proj = stack.enter_context(tc.psum_pool(name="psum_proj", bufs=4))
         psum_score = stack.enter_context(tc.psum_pool(name="psum_score", bufs=4))
         stack.enter_context(tc.manual_schedule())
@@ -49,8 +50,8 @@ def tile_coattlayer_pa_kernel(tc, x, Wq, bq, Wk, bk, out):
         x_sb = keep.tile([P, IMAGES, PACK, PIXELS], BF16)
         wk_rows = keep.tile([P, PACK * CHANNELS], BF16)
         wq_rows = keep.tile([P, PACK * CHANNELS], BF16)
-        nc.sync.dma_start(out=x_sb[:, 0:2], in_=x_view[:, 0:2])
         nc.sync.dma_start(out=wk_rows[:], in_=Wk.rearrange("(p t) c -> p (t c)", t=PACK))
+        nc.sync.dma_start(out=x_sb[:, 0:2], in_=x_view[:, 0:2])
         nc.sync.dma_start(out=wq_rows[:], in_=Wq.rearrange("(p t) c -> p (t c)", t=PACK))
         for pair in range(1, PAIRS):
             nc.sync.dma_start(out=x_sb[:, 2 * pair : 2 * pair + 2], in_=x_view[:, 2 * pair : 2 * pair + 2])
@@ -170,8 +171,8 @@ def tile_coattlayer_pa_kernel(tc, x, Wq, bq, Wk, bk, out):
                 in_=grouped[:].rearrange("p n t -> p (n t)"),
             )
 
-        units = [(chunk, pair) for pair in range(PAIRS) for chunk in range(CHUNKS_PER_PAIR)]
-        units += [(chunk, pair) for chunk in range(CHUNKS_PER_PAIR, CHUNKS) for pair in range(PAIRS)]
+        early_units = [(chunk, pair) for pair in range(PAIRS) for chunk in range(EARLY_CHUNKS)]
+        units = early_units + [(chunk, pair) for chunk in range(EARLY_CHUNKS, CHUNKS) for pair in range(PAIRS)]
         banks = {}
 
         def score_pass(n):
@@ -268,7 +269,10 @@ def tile_coattlayer_pa_kernel(tc, x, Wq, bq, Wk, bk, out):
 
         def endings(n):
             for image in range(IMAGES):
-                last_unit = max(CHUNKS_PER_PAIR, 2 * image + 2) * PAIRS - 1
+                if 2 * image < EARLY_CHUNKS:
+                    last_unit = (PAIRS - 1) * EARLY_CHUNKS + 2 * image + 1
+                else:
+                    last_unit = (2 * image + 2) * PAIRS - 1
                 if n == last_unit:
                     add_up(image)
                 if n == last_unit + SPREAD_LAG:
@@ -288,43 +292,40 @@ def tile_coattlayer_pa_kernel(tc, x, Wq, bq, Wk, bk, out):
         nc.vector.quantize_mx(out=wq_codes[:].bitcast(FP8X4), scales=wq_scales[:], in_=wq_grouped[:])
         q0_planes = project(side_q, 0)
         quantise_x(1, x_grouped)
-        k1_planes = project(side_k, 1)
+        q1_planes = project(side_q, 1)
         x_grouped = regroup_x(2)
         k0_grouped = regroup_on_vector(k0_planes)
+        k1_planes = project(side_k, 1)
         quantise_x(2, x_grouped)
-        k2_planes = project(side_k, 2)
-        waiting = {("k", 2): regroup_on_gpsimd(k2_planes)}
         quantise(side_k, 0, k0_grouped)
         q0_grouped = regroup_on_vector(q0_planes)
         x_grouped = regroup_x(3)
         quantise(side_q, 0, q0_grouped)
         for n in range(LEAD):
             score_pass(n)
+        waiting = {("q", 1): regroup_on_vector(q1_planes)}
         quantise_x(3, x_grouped)
+        waiting[("k", 1)] = regroup_on_vector(k1_planes)
 
         sides = {"k": side_k, "q": side_q}
-        carried = (("k", 3), ("q", 1), ("q", 2), ("q", 3))
-        for block in range(PAIRS):
-            name, pair = carried[block]
-            planes = new_planes()
-            for chunk in range(CHUNKS_PER_PAIR):
-                n = block * CHUNKS_PER_PAIR + chunk
-                project_pass(sides[name], pair, planes, chunk)
-                if block == 0 and chunk == 0:
-                    waiting[("k", 1)] = regroup_on_vector(k1_planes)
-                if chunk == LEAD:
-                    due = ("k", block + 1) if block + 1 < PAIRS else ("q", 1)
-                    quantise(sides[due[0]], due[1], waiting[due])
-                score_pass(n + LEAD)
-                take_maxima(n)
-                endings(n)
-            waiting[(name, pair)] = regroup_on_gpsimd(planes)
-
-        for n in range(CHUNKS_PER_PAIR * PAIRS, len(units) + GATE_LAG + 1):
-            if (n + LEAD) % (CHUNKS_PER_PAIR * PAIRS) == 0 and n + LEAD < len(units):
-                due = ("q", (n + LEAD) // (CHUNKS_PER_PAIR * PAIRS))
-                quantise(side_q, due[1], waiting[due])
-            score_pass(n + LEAD)
+        carried = (("k", 2), ("k", 3), ("q", 2), ("q", 3))
+        for n in range(len(units) + GATE_LAG + 1):
+            if n < len(carried) * PACK:
+                name, pair = carried[n // PACK]
+                if n % PACK == 0:
+                    planes = new_planes()
+                project_pass(sides[name], pair, planes, n % PACK)
+                if n % PACK == PACK - 1:
+                    waiting[(name, pair)] = regroup_on_gpsimd(planes)
+            ahead = n + LEAD
+            if ahead == CHUNKS_PER_PAIR:
+                quantise(side_q, 1, waiting[("q", 1)])
+            if ahead % EARLY_CHUNKS == 0 and ahead < len(early_units):
+                quantise(side_k, ahead // EARLY_CHUNKS, waiting[("k", ahead // EARLY_CHUNKS)])
+            if ahead == len(early_units):
+                quantise(side_q, 2, waiting[("q", 2)])
+                quantise(side_q, 3, waiting[("q", 3)])
+            score_pass(ahead)
             if n < len(units):
                 take_maxima(n)
             endings(n)

@@ -30,6 +30,8 @@ LEAD = 3
 SPREAD_LAG = 1
 EXP_LAG = 4
 GATE_LAG = 7
+QUANT_FIRST = 10
+QUANT_EVERY = 7
 
 FLOPS = 2 * 2 * ALL_PIXELS * CHANNELS * CHANNELS + 2 * ALL_PIXELS * ALL_PIXELS * CHANNELS
 
@@ -103,11 +105,10 @@ def tile_coattlayer_pa_kernel(tc, x, Wq, bq, Wk, bk, out):
 
         def regroup_x(pair):
             grouped = stage.tile([P, 2, PIXELS, PACK], BF16, tag="x_grouped", bufs=PAIRS, align_bytes=64)
-            for i in range(2):
-                nc.vector.tensor_copy(
-                    out=grouped[:, i].rearrange("p (c r) j -> p c j r", r=4),
-                    in_=x_sb[:, 2 * pair + i].rearrange("p j (c r) -> p c j r", r=4),
-                )
+            nc.vector.tensor_copy(
+                out=grouped[:].rearrange("p i (c r) j -> p i c j r", r=4),
+                in_=x_sb[:, 2 * pair : 2 * pair + 2].rearrange("p i j (c r) -> p i c j r", r=4),
+            )
             return grouped
 
         def quantise_x(pair, grouped):
@@ -151,17 +152,15 @@ def tile_coattlayer_pa_kernel(tc, x, Wq, bq, Wk, bk, out):
             return grouped
 
         def regroup_on_gpsimd(planes):
-            grouped = stage.tile([P, PAIR, PACK], BF16, tag="grouped", bufs=4, align_bytes=64)
-            for i in range(2):
-                pix = slice(i * PIXELS, (i + 1) * PIXELS)
-                nc.gpsimd.tensor_scalar(
-                    out=grouped[:, pix, :],
-                    in0=planes[:, :, pix].rearrange("p t n -> p n t"),
-                    scalar1=1.0,
-                    scalar2=0.0,
-                    op0=ALU.mult,
-                    op1=ALU.add,
-                )
+            grouped = stage.tile([P, PAIR, PACK], BF16, tag="carried_grouped", bufs=1, align_bytes=64)
+            nc.gpsimd.tensor_scalar(
+                out=grouped[:],
+                in0=planes[:].rearrange("p t n -> p n t"),
+                scalar1=1.0,
+                scalar2=0.0,
+                op0=ALU.mult,
+                op1=ALU.add,
+            )
             return grouped
 
         def quantise(side, pair, grouped):
@@ -303,29 +302,32 @@ def tile_coattlayer_pa_kernel(tc, x, Wq, bq, Wk, bk, out):
         quantise(side_q, 0, q0_grouped)
         for n in range(LEAD):
             score_pass(n)
-        waiting = {("q", 1): regroup_on_vector(q1_planes)}
+        q1_grouped = regroup_on_vector(q1_planes)
         quantise_x(3, x_grouped)
-        waiting[("k", 1)] = regroup_on_vector(k1_planes)
+        k1_grouped = regroup_on_vector(k1_planes)
 
         sides = {"k": side_k, "q": side_q}
         carried = (("k", 2), ("k", 3), ("q", 2), ("q", 3))
+        carried_planes = {}
         for n in range(len(units) + GATE_LAG + 1):
             if n < len(carried) * PACK:
                 name, pair = carried[n // PACK]
                 if n % PACK == 0:
-                    planes = new_planes()
-                project_pass(sides[name], pair, planes, n % PACK)
-                if n % PACK == PACK - 1:
-                    waiting[(name, pair)] = regroup_on_gpsimd(planes)
-            ahead = n + LEAD
-            if ahead == CHUNKS_PER_PAIR:
-                quantise(side_q, 1, waiting[("q", 1)])
-            if ahead % EARLY_CHUNKS == 0 and ahead < len(early_units):
-                quantise(side_k, ahead // EARLY_CHUNKS, waiting[("k", ahead // EARLY_CHUNKS)])
-            if ahead == len(early_units):
-                quantise(side_q, 2, waiting[("q", 2)])
-                quantise(side_q, 3, waiting[("q", 3)])
-            score_pass(ahead)
+                    carried_planes[n // PACK] = new_planes()
+                project_pass(sides[name], pair, carried_planes[n // PACK], n % PACK)
+            if n == PACK - 1:
+                carried_grouped = regroup_on_gpsimd(carried_planes[0])
+            if n == 1:
+                quantise(side_q, 1, q1_grouped)
+            if n == 3:
+                quantise(side_k, 1, k1_grouped)
+            turn = (n - QUANT_FIRST) // QUANT_EVERY
+            if (n - QUANT_FIRST) % QUANT_EVERY == 0 and 0 <= turn < len(carried):
+                name, pair = carried[turn]
+                quantise(sides[name], pair, carried_grouped)
+                if turn + 1 < len(carried):
+                    carried_grouped = regroup_on_gpsimd(carried_planes[turn + 1])
+            score_pass(n + LEAD)
             if n < len(units):
                 take_maxima(n)
             endings(n)

@@ -27,11 +27,20 @@ GATE_SCALE = 1.0 / (IMAGES * math.sqrt(CHANNELS))
 
 EARLY_CHUNKS = 2 * CHUNKS_PER_PAIR
 LEAD = 3
+EARLY_DELAY = 3
 SPREAD_LAG = 1
-EXP_LAG = 4
-GATE_LAG = 7
+EXP_LAG = 3
+GATE_LAG = 6
 QUANT_FIRST = 10
 QUANT_EVERY = 7
+
+STAGES = (
+    (range(4), (0,)),
+    (range(4), (1,)),
+    (range(4, 8), (0, 1)),
+    (range(8), (2,)),
+    (range(8), (3,)),
+) + tuple(((chunk,), range(PAIRS)) for chunk in range(8, CHUNKS))
 
 FLOPS = 2 * 2 * ALL_PIXELS * CHANNELS * CHANNELS + 2 * ALL_PIXELS * ALL_PIXELS * CHANNELS
 
@@ -52,15 +61,16 @@ def tile_coattlayer_pa_kernel(tc, x, Wq, bq, Wk, bk, out):
         x_sb = keep.tile([P, IMAGES, PACK, PIXELS], BF16)
         wk_rows = keep.tile([P, PACK * CHANNELS], BF16)
         wq_rows = keep.tile([P, PACK * CHANNELS], BF16)
-        nc.sync.dma_start(out=wk_rows[:], in_=Wk.rearrange("(p t) c -> p (t c)", t=PACK))
-        nc.sync.dma_start(out=x_sb[:, 0:2], in_=x_view[:, 0:2])
-        nc.sync.dma_start(out=wq_rows[:], in_=Wq.rearrange("(p t) c -> p (t c)", t=PACK))
-        for pair in range(1, PAIRS):
-            nc.sync.dma_start(out=x_sb[:, 2 * pair : 2 * pair + 2], in_=x_view[:, 2 * pair : 2 * pair + 2])
         bk_raw = keep.tile([P, PACK], BF16)
         bq_raw = keep.tile([P, PACK], BF16)
         nc.scalar.dma_start(out=bk_raw[:], in_=bk.rearrange("(p t) -> p t", t=PACK))
         nc.scalar.dma_start(out=bq_raw[:], in_=bq.rearrange("(p t) -> p t", t=PACK))
+        nc.sync.dma_start(out=wk_rows[:], in_=Wk.rearrange("(p t) c -> p (t c)", t=PACK))
+        for image in range(2):
+            nc.sync.dma_start(out=x_sb[:, image : image + 1], in_=x_view[:, image : image + 1])
+        nc.sync.dma_start(out=wq_rows[:], in_=Wq.rearrange("(p t) c -> p (t c)", t=PACK))
+        for pair in range(1, PAIRS):
+            nc.sync.dma_start(out=x_sb[:, 2 * pair : 2 * pair + 2], in_=x_view[:, 2 * pair : 2 * pair + 2])
 
         ident = keep.tile([P, P], F32)
         make_identity(nc, ident[:])
@@ -80,45 +90,74 @@ def tile_coattlayer_pa_kernel(tc, x, Wq, bq, Wk, bk, out):
         q_codes = keep.tile([P, ALL_PIXELS], U32, align_bytes=64)
         q_scales = keep.tile([P, ALL_PIXELS], U8, align_bytes=64)
         best = keep.tile([P, CHUNKS, IMAGES], F32)
-        side_k = {"w_codes": wk_codes, "w_scales": wk_scales, "bias": bk_f32, "codes": k_codes, "scales": k_scales}
-        side_q = {"w_codes": wq_codes, "w_scales": wq_scales, "bias": bq_f32, "codes": q_codes, "scales": q_scales}
+        sides = {}
+        sides["k"] = {"w_codes": wk_codes, "w_scales": wk_scales, "bias": bk_f32, "codes": k_codes, "scales": k_scales}
+        sides["q"] = {"w_codes": wq_codes, "w_scales": wq_scales, "bias": bq_f32, "codes": q_codes, "scales": q_scales}
 
         def pair_cols(pair):
             return slice(pair * PAIR, (pair + 1) * PAIR)
 
-        def turn_weight(rows):
+        def turn_half(rows, grouped, half, on_vector):
             words = rows[:].bitcast(F32).rearrange("p (t q u) -> p t u q", t=PACK, u=2)
-            grouped = stage.tile([P, PACK * CHANNELS], BF16, tag="w_grouped", align_bytes=64)
             grouped_words = grouped[:].bitcast(F32).rearrange("p (t d u) -> p t d u", t=PACK, u=2)
-            for half in range(2):
-                turned = psum_score.tile([P, 2, 2, P], F32, tag="score")
-                for a in range(2):
-                    for u in range(2):
-                        nc.tensor.transpose(
-                            out=turned[:, a, u, :], in_=words[:, 2 * half + a, u, :], identity=ident[:]
-                        )
-                nc.scalar.copy(
-                    out=grouped_words[:, 2 * half : 2 * half + 2],
-                    in_=turned[:].rearrange("p a u d -> p a d u"),
-                )
+            turned = psum_score.tile([P, 2, 2, P], F32, tag="score")
+            for a in range(2):
+                for u in range(2):
+                    nc.tensor.transpose(out=turned[:, a, u, :], in_=words[:, 2 * half + a, u, :], identity=ident[:])
+            target = grouped_words[:, 2 * half : 2 * half + 2]
+            source = turned[:].rearrange("p a u d -> p a d u")
+            if on_vector:
+                nc.vector.tensor_copy(out=target, in_=source)
+            else:
+                nc.scalar.copy(out=target, in_=source)
+
+        def quantise_w_half(side, grouped, half):
+            cols = slice(half * 2 * P, (half + 1) * 2 * P)
+            nc.vector.quantize_mx(
+                out=side["w_codes"][:, cols].bitcast(FP8X4),
+                scales=side["w_scales"][:, cols],
+                in_=grouped[:, half * 2 * P * PACK : (half + 1) * 2 * P * PACK],
+            )
+
+        def new_w_grouped():
+            grouped = stage.tile([P, PACK * CHANNELS], BF16, tag="w_grouped", align_bytes=64)
             return grouped
 
-        def regroup_x(pair):
-            grouped = stage.tile([P, 2, PIXELS, PACK], BF16, tag="x_grouped", bufs=PAIRS, align_bytes=64)
+        x_grouped = {}
+
+        def regroup_x(first, count):
+            grouped = stage.tile([P, count, PIXELS, PACK], BF16, tag="x_grouped", bufs=PAIRS, align_bytes=64)
             nc.vector.tensor_copy(
                 out=grouped[:].rearrange("p i (c r) j -> p i c j r", r=4),
-                in_=x_sb[:, 2 * pair : 2 * pair + 2].rearrange("p i j (c r) -> p i c j r", r=4),
+                in_=x_sb[:, first : first + count].rearrange("p i j (c r) -> p i c j r", r=4),
             )
-            return grouped
+            x_grouped[first] = grouped
 
-        def quantise_x(pair, grouped):
+        def regroup_x_shared(first):
+            grouped = stage.tile([P, 2, PIXELS, PACK], BF16, tag="x_grouped", bufs=PAIRS, align_bytes=64)
+            nc.scalar.copy(
+                out=grouped[:, 0, :, :].rearrange("p (c r) j -> p c j r", r=4),
+                in_=x_sb[:, first, :, :].rearrange("p j (c r) -> p c j r", r=4),
+            )
+            nc.gpsimd.tensor_scalar(
+                out=grouped[:, 1, :, :],
+                in0=x_sb[:, first + 1, :, :].rearrange("p j n -> p n j"),
+                scalar1=1.0,
+                scalar2=0.0,
+                op0=ALU.mult,
+                op1=ALU.add,
+            )
+            x_grouped[first] = grouped
+
+        def quantise_x(first, count):
+            cols = slice(first * PIXELS, (first + count) * PIXELS)
             nc.vector.quantize_mx(
-                out=x_codes[:, pair_cols(pair)].bitcast(FP8X4),
-                scales=x_scales[:, pair_cols(pair)],
-                in_=grouped[:].rearrange("p i w j -> p (i w j)"),
+                out=x_codes[:, cols].bitcast(FP8X4),
+                scales=x_scales[:, cols],
+                in_=x_grouped[first][:].rearrange("p i w j -> p (i w j)"),
             )
 
-        def project_pass(side, pair, planes, t):
+        def project_pass(side, pair, planes, t, on_vector):
             acc = psum_proj.tile([P, PAIR], F32, tag="proj")
             nc.tensor.matmul_mx(
                 out=acc[:],
@@ -129,54 +168,75 @@ def tile_coattlayer_pa_kernel(tc, x, Wq, bq, Wk, bk, out):
                 start=True,
                 stop=True,
             )
-            nc.scalar.activation(
-                out=planes[:, t, :], in_=acc[:], func=ACT.Identity, bias=side["bias"][:, t : t + 1], scale=1.0
-            )
+            bias = side["bias"][:, t : t + 1]
+            if on_vector:
+                nc.vector.tensor_scalar(
+                    out=planes[:, t, :], in0=acc[:], scalar1=bias, scalar2=None, op0=ALU.add
+                )
+            else:
+                nc.scalar.activation(out=planes[:, t, :], in_=acc[:], func=ACT.Identity, bias=bias, scale=1.0)
 
-        def new_planes():
-            planes = stage.tile([P, PACK, PAIR], BF16, tag="planes", bufs=3)
-            return planes
+        items = {}
 
-        def project(side, pair):
-            planes = new_planes()
-            for t in range(PACK):
-                project_pass(side, pair, planes, t)
-            return planes
+        def project(name, pair, passes, on_vector=False):
+            for t in passes:
+                if (name, pair) not in items:
+                    planes = stage.tile([P, PACK, PAIR], BF16, tag="planes", bufs=3)
+                    items[name, pair] = planes
+                project_pass(sides[name], pair, items[name, pair], t, on_vector)
 
-        def regroup_on_vector(planes):
+        def regroup_on_vector(name, pair):
+            planes = items[name, pair]
             grouped = stage.tile([P, PAIR, PACK], BF16, tag="grouped", bufs=4, align_bytes=64)
             nc.vector.tensor_copy(
                 out=grouped[:].rearrange("p (c r) t -> p c t r", r=4),
                 in_=planes[:].rearrange("p t (c r) -> p c t r", r=4),
             )
-            return grouped
+            items[name, pair] = grouped
 
-        def regroup_on_gpsimd(planes):
-            grouped = stage.tile([P, PAIR, PACK], BF16, tag="carried_grouped", bufs=1, align_bytes=64)
+        def regroup_shared(name, pair):
+            planes = items[name, pair]
+            grouped = stage.tile([P, PAIR, PACK], BF16, tag="grouped", bufs=4, align_bytes=64)
+            nc.scalar.copy(
+                out=grouped[:, 0:PIXELS, :].rearrange("p (c r) t -> p c t r", r=4),
+                in_=planes[:, :, 0:PIXELS].rearrange("p t (c r) -> p c t r", r=4),
+            )
             nc.gpsimd.tensor_scalar(
-                out=grouped[:],
-                in0=planes[:].rearrange("p t n -> p n t"),
+                out=grouped[:, PIXELS:PAIR, :],
+                in0=planes[:, :, PIXELS:PAIR].rearrange("p t n -> p n t"),
                 scalar1=1.0,
                 scalar2=0.0,
                 op0=ALU.mult,
                 op1=ALU.add,
             )
-            return grouped
+            items[name, pair] = grouped
 
-        def quantise(side, pair, grouped):
+        def quantise(name, pair, first=0, count=PAIR):
+            side = sides[name]
+            cols = slice(pair * PAIR + first, pair * PAIR + first + count)
             nc.vector.quantize_mx(
-                out=side["codes"][:, pair_cols(pair)].bitcast(FP8X4),
-                scales=side["scales"][:, pair_cols(pair)],
-                in_=grouped[:].rearrange("p n t -> p (n t)"),
+                out=side["codes"][:, cols].bitcast(FP8X4),
+                scales=side["scales"][:, cols],
+                in_=items[name, pair][:, first : first + count, :].rearrange("p n t -> p (n t)"),
             )
+            if name == "k":
+                ready.add(("k", pair))
+            else:
+                for chunk in range(pair * CHUNKS_PER_PAIR + first // P, pair * CHUNKS_PER_PAIR + (first + count) // P):
+                    ready.add(("q", chunk))
 
-        early_units = [(chunk, pair) for pair in range(PAIRS) for chunk in range(EARLY_CHUNKS)]
-        units = early_units + [(chunk, pair) for chunk in range(EARLY_CHUNKS, CHUNKS) for pair in range(PAIRS)]
+        ready = set()
+
+        units = []
+        for chunks, pairs in STAGES:
+            units += [(chunk, pair) for pair in pairs for chunk in chunks]
         banks = {}
 
+        def available(n):
+            chunk, pair = units[n]
+            return ("q", chunk) in ready and ("k", pair) in ready
+
         def score_pass(n):
-            if n >= len(units):
-                return
             chunk, pair = units[n]
             acc = psum_score.tile([P, PAIR], F32, tag="score")
             nc.tensor.matmul_mx(
@@ -206,9 +266,15 @@ def tile_coattlayer_pa_kernel(tc, x, Wq, bq, Wk, bk, out):
 
         def add_up(image):
             total = small.tile([P, 2], F32, tag="total")
-            nc.vector.tensor_reduce(
-                out=total[:], in_=best[:, 2 * image : 2 * image + 2, :], axis=AXIS_X, op=ALU.add
-            )
+            scaled = small.tile([P, 2, IMAGES], F32, tag="scaled")
+            for h in range(2):
+                nc.scalar.activation(
+                    out=scaled[:, h, :],
+                    in_=best[:, 2 * image + h, :],
+                    func=ACT.Copy,
+                    scale=-GATE_SCALE,
+                    accum_out=total[:, h : h + 1],
+                )
             totals[image] = total
 
         def spread_out(image):
@@ -222,10 +288,8 @@ def tile_coattlayer_pa_kernel(tc, x, Wq, bq, Wk, bk, out):
             spreads[image] = spread
 
         def exponentials(image):
-            top = small.tile([P, 1], F32, tag="top")
-            nc.vector.tensor_reduce(out=top[:], in_=spreads[image][:], axis=AXIS_X, op=ALU.max)
             shift = small.tile([P, 1], F32, tag="shift")
-            nc.scalar.mul(out=shift[:], in_=top[:], mul=-GATE_SCALE)
+            nc.vector.tensor_reduce(out=shift[:], in_=spreads[image][:], axis=AXIS_X, op=ALU.min)
             numer = small.tile([P, PIXELS], F32, tag="numer")
             denom = small.tile([P, 1], F32, tag="denom")
             nc.scalar.activation(
@@ -233,7 +297,7 @@ def tile_coattlayer_pa_kernel(tc, x, Wq, bq, Wk, bk, out):
                 in_=spreads[image][:],
                 func=ACT.Exp,
                 bias=shift[:, 0:1],
-                scale=GATE_SCALE,
+                scale=-1.0,
                 accum_out=denom[:],
             )
             numers[image] = numer
@@ -254,13 +318,13 @@ def tile_coattlayer_pa_kernel(tc, x, Wq, bq, Wk, bk, out):
                 )
                 nc.sync.dma_start(out=out_view[image], in_=product[:])
             else:
-                for half in range(2):
-                    rows = slice(2 * half, 2 * half + 2)
+                for j in range(PACK):
+                    rows = slice(j, j + 1)
                     nc.vector.scalar_tensor_tensor(
                         out=product[:, rows, :],
                         in0=x_sb[:, image, rows, :],
                         scalar=inverse[:, 0:1],
-                        in1=numers[image][:].unsqueeze(1).to_broadcast([P, 2, PIXELS]),
+                        in1=numers[image][:].unsqueeze(1).to_broadcast([P, 1, PIXELS]),
                         op0=ALU.mult,
                         op1=ALU.mult,
                     )
@@ -268,10 +332,7 @@ def tile_coattlayer_pa_kernel(tc, x, Wq, bq, Wk, bk, out):
 
         def endings(n):
             for image in range(IMAGES):
-                if 2 * image < EARLY_CHUNKS:
-                    last_unit = (PAIRS - 1) * EARLY_CHUNKS + 2 * image + 1
-                else:
-                    last_unit = (2 * image + 2) * PAIRS - 1
+                last_unit = max(units.index((2 * image + h, pair)) for h in range(2) for pair in range(PAIRS))
                 if n == last_unit:
                     add_up(image)
                 if n == last_unit + SPREAD_LAG:
@@ -281,53 +342,62 @@ def tile_coattlayer_pa_kernel(tc, x, Wq, bq, Wk, bk, out):
                 if n == last_unit + GATE_LAG:
                     gate_and_store(image)
 
-        x_grouped = regroup_x(0)
-        quantise_x(0, x_grouped)
-        wk_grouped = turn_weight(wk_rows)
-        wq_grouped = turn_weight(wq_rows)
-        nc.vector.quantize_mx(out=wk_codes[:].bitcast(FP8X4), scales=wk_scales[:], in_=wk_grouped[:])
-        k0_planes = project(side_k, 0)
-        x_grouped = regroup_x(1)
-        nc.vector.quantize_mx(out=wq_codes[:].bitcast(FP8X4), scales=wq_scales[:], in_=wq_grouped[:])
-        q0_planes = project(side_q, 0)
-        quantise_x(1, x_grouped)
-        q1_planes = project(side_q, 1)
-        x_grouped = regroup_x(2)
-        k0_grouped = regroup_on_vector(k0_planes)
-        k1_planes = project(side_k, 1)
-        quantise_x(2, x_grouped)
-        quantise(side_k, 0, k0_grouped)
-        q0_grouped = regroup_on_vector(q0_planes)
-        x_grouped = regroup_x(3)
-        quantise(side_q, 0, q0_grouped)
-        for n in range(LEAD):
-            score_pass(n)
-        q1_grouped = regroup_on_vector(q1_planes)
-        quantise_x(3, x_grouped)
-        k1_grouped = regroup_on_vector(k1_planes)
+        wk_grouped = new_w_grouped()
+        wq_grouped = new_w_grouped()
+        turn_half(wk_rows, wk_grouped, 0, on_vector=False)
+        turn_half(wk_rows, wk_grouped, 1, on_vector=False)
+        regroup_x(0, 1)
+        quantise_x(0, 1)
+        regroup_x(1, 1)
+        quantise_x(1, 1)
+        quantise_w_half(sides["k"], wk_grouped, 0)
+        quantise_w_half(sides["k"], wk_grouped, 1)
+        turn_half(wq_rows, wq_grouped, 0, on_vector=False)
+        turn_half(wq_rows, wq_grouped, 1, on_vector=False)
+        project("k", 0, range(3))
+        regroup_x(2, 2)
+        quantise_w_half(sides["q"], wq_grouped, 0)
+        quantise_w_half(sides["q"], wq_grouped, 1)
+        quantise_x(2, 2)
+        project("k", 0, (3,), on_vector=True)
+        project("q", 0, (3,), on_vector=True)
+        project("q", 0, range(3))
+        regroup_on_vector("k", 0)
+        project("k", 1, range(4))
+        quantise("k", 0)
+        regroup_on_vector("q", 0)
+        regroup_shared("k", 1)
+        project("q", 1, range(4))
+        quantise("q", 0, 0, PIXELS)
+        score_pass(0)
+        score_pass(1)
+        quantise("q", 0, PIXELS, PIXELS)
 
-        sides = {"k": side_k, "q": side_q}
-        carried = (("k", 2), ("k", 3), ("q", 2), ("q", 3))
-        carried_planes = {}
+        before = {
+            3: [lambda: quantise("k", 1)],
+            7: [lambda: quantise("q", 1), lambda: quantise_x(4, 2)],
+            9: [lambda: quantise_x(6, 2)],
+            15: [lambda: quantise("k", 2)],
+            23: [lambda: quantise("k", 3)],
+            26: [lambda: quantise("q", 2)],
+            40: [lambda: quantise("q", 3)],
+        }
+        after = {
+            0: [lambda: regroup_shared("q", 1), lambda: regroup_x_shared(4), lambda: regroup_x_shared(6)],
+            7: [lambda: project("k", 2, range(4)), lambda: regroup_shared("k", 2)],
+            12: [lambda: project("k", 3, range(4)), lambda: regroup_shared("k", 3)],
+            16: [lambda: project("q", 2, range(4)), lambda: regroup_shared("q", 2)],
+            20: [lambda: project("q", 3, range(4)), lambda: regroup_shared("q", 3)],
+        }
+        issued = 2
         for n in range(len(units) + GATE_LAG + 1):
-            if n < len(carried) * PACK:
-                name, pair = carried[n // PACK]
-                if n % PACK == 0:
-                    carried_planes[n // PACK] = new_planes()
-                project_pass(sides[name], pair, carried_planes[n // PACK], n % PACK)
-            if n == PACK - 1:
-                carried_grouped = regroup_on_gpsimd(carried_planes[0])
-            if n == 1:
-                quantise(side_q, 1, q1_grouped)
-            if n == 3:
-                quantise(side_k, 1, k1_grouped)
-            turn = (n - QUANT_FIRST) // QUANT_EVERY
-            if (n - QUANT_FIRST) % QUANT_EVERY == 0 and 0 <= turn < len(carried):
-                name, pair = carried[turn]
-                quantise(sides[name], pair, carried_grouped)
-                if turn + 1 < len(carried):
-                    carried_grouped = regroup_on_gpsimd(carried_planes[turn + 1])
-            score_pass(n + LEAD)
+            for step in before.get(n, []):
+                step()
+            while issued < min(n + LEAD + 1, len(units)) and available(issued):
+                score_pass(issued)
+                issued += 1
             if n < len(units):
                 take_maxima(n)
+            for step in after.get(n, []):
+                step()
             endings(n)

@@ -27,10 +27,10 @@ GATE_SCALE = 1.0 / (IMAGES * math.sqrt(CHANNELS))
 
 EARLY_CHUNKS = 2 * CHUNKS_PER_PAIR
 LEAD = 3
-EARLY_DELAY = 3
+EARLY_DELAY = 5
 SPREAD_LAG = 1
 EXP_LAG = 3
-GATE_LAG = 6
+GATE_LAG = 5
 QUANT_FIRST = 10
 QUANT_EVERY = 7
 
@@ -125,36 +125,35 @@ def tile_coattlayer_pa_kernel(tc, x, Wq, bq, Wk, bk, out):
 
         x_grouped = {}
 
-        def regroup_x(first, count):
-            grouped = stage.tile([P, count, PIXELS, PACK], BF16, tag="x_grouped", bufs=PAIRS, align_bytes=64)
-            nc.vector.tensor_copy(
-                out=grouped[:].rearrange("p i (c r) j -> p i c j r", r=4),
-                in_=x_sb[:, first : first + count].rearrange("p i j (c r) -> p i c j r", r=4),
-            )
-            x_grouped[first] = grouped
+        def interleave(engine, grouped, rows):
+            if engine == "gpsimd":
+                nc.gpsimd.tensor_scalar(
+                    out=grouped,
+                    in0=rows.rearrange("p j n -> p n j"),
+                    scalar1=1.0,
+                    scalar2=0.0,
+                    op0=ALU.mult,
+                    op1=ALU.add,
+                )
+                return
+            target = grouped.rearrange("p (c r) j -> p c j r", r=4)
+            source = rows.rearrange("p j (c r) -> p c j r", r=4)
+            if engine == "scalar":
+                nc.scalar.copy(out=target, in_=source)
+            else:
+                nc.vector.tensor_copy(out=target, in_=source)
 
-        def regroup_x_shared(first):
-            grouped = stage.tile([P, 2, PIXELS, PACK], BF16, tag="x_grouped", bufs=PAIRS, align_bytes=64)
-            nc.scalar.copy(
-                out=grouped[:, 0, :, :].rearrange("p (c r) j -> p c j r", r=4),
-                in_=x_sb[:, first, :, :].rearrange("p j (c r) -> p c j r", r=4),
-            )
-            nc.gpsimd.tensor_scalar(
-                out=grouped[:, 1, :, :],
-                in0=x_sb[:, first + 1, :, :].rearrange("p j n -> p n j"),
-                scalar1=1.0,
-                scalar2=0.0,
-                op0=ALU.mult,
-                op1=ALU.add,
-            )
-            x_grouped[first] = grouped
+        def regroup_x(image, engine):
+            grouped = stage.tile([P, PIXELS, PACK], BF16, tag="x_grouped", bufs=IMAGES, align_bytes=64)
+            interleave(engine, grouped[:], x_sb[:, image, :, :])
+            x_grouped[image] = grouped
 
-        def quantise_x(first, count):
-            cols = slice(first * PIXELS, (first + count) * PIXELS)
+        def quantise_x(image):
+            cols = slice(image * PIXELS, (image + 1) * PIXELS)
             nc.vector.quantize_mx(
                 out=x_codes[:, cols].bitcast(FP8X4),
                 scales=x_scales[:, cols],
-                in_=x_grouped[first][:].rearrange("p i w j -> p (i w j)"),
+                in_=x_grouped[image][:].rearrange("p w j -> p (w j)"),
             )
 
         def project_pass(side, pair, planes, t, on_vector):
@@ -176,54 +175,43 @@ def tile_coattlayer_pa_kernel(tc, x, Wq, bq, Wk, bk, out):
             else:
                 nc.scalar.activation(out=planes[:, t, :], in_=acc[:], func=ACT.Identity, bias=bias, scale=1.0)
 
-        items = {}
+        all_planes = {}
+        grouped_halves = {}
 
         def project(name, pair, passes, on_vector=False):
             for t in passes:
-                if (name, pair) not in items:
+                if (name, pair) not in all_planes:
                     planes = stage.tile([P, PACK, PAIR], BF16, tag="planes", bufs=3)
-                    items[name, pair] = planes
-                project_pass(sides[name], pair, items[name, pair], t, on_vector)
+                    all_planes[name, pair] = planes
+                project_pass(sides[name], pair, all_planes[name, pair], t, on_vector)
 
-        def regroup_on_vector(name, pair):
-            planes = items[name, pair]
-            grouped = stage.tile([P, PAIR, PACK], BF16, tag="grouped", bufs=4, align_bytes=64)
-            nc.vector.tensor_copy(
-                out=grouped[:].rearrange("p (c r) t -> p c t r", r=4),
-                in_=planes[:].rearrange("p t (c r) -> p c t r", r=4),
-            )
-            items[name, pair] = grouped
+        def regroup(name, pair, half, engine):
+            if half == 0:
+                grouped = stage.tile([P, PIXELS, PACK], BF16, tag="grouped_0", bufs=4, align_bytes=64)
+            else:
+                grouped = stage.tile([P, PIXELS, PACK], BF16, tag="grouped_1", bufs=1, align_bytes=64)
+            cols = slice(half * PIXELS, (half + 1) * PIXELS)
+            interleave(engine, grouped[:], all_planes[name, pair][:, :, cols])
+            grouped_halves[name, pair, half] = grouped
 
         def regroup_shared(name, pair):
-            planes = items[name, pair]
-            grouped = stage.tile([P, PAIR, PACK], BF16, tag="grouped", bufs=4, align_bytes=64)
-            nc.scalar.copy(
-                out=grouped[:, 0:PIXELS, :].rearrange("p (c r) t -> p c t r", r=4),
-                in_=planes[:, :, 0:PIXELS].rearrange("p t (c r) -> p c t r", r=4),
-            )
-            nc.gpsimd.tensor_scalar(
-                out=grouped[:, PIXELS:PAIR, :],
-                in0=planes[:, :, PIXELS:PAIR].rearrange("p t n -> p n t"),
-                scalar1=1.0,
-                scalar2=0.0,
-                op0=ALU.mult,
-                op1=ALU.add,
-            )
-            items[name, pair] = grouped
+            regroup(name, pair, 0, "scalar")
+            regroup(name, pair, 1, "gpsimd")
 
-        def quantise(name, pair, first=0, count=PAIR):
+        def quantise_half(name, pair, half):
             side = sides[name]
-            cols = slice(pair * PAIR + first, pair * PAIR + first + count)
+            image = 2 * pair + half
+            cols = slice(image * PIXELS, (image + 1) * PIXELS)
             nc.vector.quantize_mx(
                 out=side["codes"][:, cols].bitcast(FP8X4),
                 scales=side["scales"][:, cols],
-                in_=items[name, pair][:, first : first + count, :].rearrange("p n t -> p (n t)"),
+                in_=grouped_halves[name, pair, half][:].rearrange("p n t -> p (n t)"),
             )
-            if name == "k":
-                ready.add(("k", pair))
-            else:
-                for chunk in range(pair * CHUNKS_PER_PAIR + first // P, pair * CHUNKS_PER_PAIR + (first + count) // P):
-                    ready.add(("q", chunk))
+            ready.add((name, image))
+
+        def quantise(name, pair):
+            quantise_half(name, pair, 0)
+            quantise_half(name, pair, 1)
 
         ready = set()
 
@@ -234,7 +222,7 @@ def tile_coattlayer_pa_kernel(tc, x, Wq, bq, Wk, bk, out):
 
         def available(n):
             chunk, pair = units[n]
-            return ("q", chunk) in ready and ("k", pair) in ready
+            return ("q", chunk // 2) in ready and ("k", 2 * pair + 1) in ready
 
         def score_pass(n):
             chunk, pair = units[n]
@@ -333,6 +321,8 @@ def tile_coattlayer_pa_kernel(tc, x, Wq, bq, Wk, bk, out):
         def endings(n):
             for image in range(IMAGES):
                 last_unit = max(units.index((2 * image + h, pair)) for h in range(2) for pair in range(PAIRS))
+                if 2 * image < EARLY_CHUNKS:
+                    last_unit += EARLY_DELAY
                 if n == last_unit:
                     add_up(image)
                 if n == last_unit + SPREAD_LAG:
@@ -346,48 +336,55 @@ def tile_coattlayer_pa_kernel(tc, x, Wq, bq, Wk, bk, out):
         wq_grouped = new_w_grouped()
         turn_half(wk_rows, wk_grouped, 0, on_vector=False)
         turn_half(wk_rows, wk_grouped, 1, on_vector=False)
-        regroup_x(0, 1)
-        quantise_x(0, 1)
-        regroup_x(1, 1)
-        quantise_x(1, 1)
+        regroup_x(0, "vector")
+        regroup_x(1, "vector")
+        quantise_x(0)
+        quantise_x(1)
         quantise_w_half(sides["k"], wk_grouped, 0)
         quantise_w_half(sides["k"], wk_grouped, 1)
         turn_half(wq_rows, wq_grouped, 0, on_vector=False)
         turn_half(wq_rows, wq_grouped, 1, on_vector=False)
         project("k", 0, range(3))
-        regroup_x(2, 2)
+        regroup_x(2, "vector")
+        regroup_x(3, "vector")
         quantise_w_half(sides["q"], wq_grouped, 0)
         quantise_w_half(sides["q"], wq_grouped, 1)
-        quantise_x(2, 2)
+        quantise_x(2)
+        quantise_x(3)
         project("k", 0, (3,), on_vector=True)
         project("q", 0, (3,), on_vector=True)
         project("q", 0, range(3))
-        regroup_on_vector("k", 0)
+        regroup("k", 0, 0, "vector")
+        regroup("k", 0, 1, "vector")
         project("k", 1, range(4))
-        quantise("k", 0)
-        regroup_on_vector("q", 0)
-        regroup_shared("k", 1)
+        quantise_half("k", 0, 0)
+        quantise_half("k", 0, 1)
+        regroup("q", 0, 0, "vector")
+        regroup("q", 0, 1, "vector")
+        regroup("k", 1, 0, "scalar")
         project("q", 1, range(4))
-        quantise("q", 0, 0, PIXELS)
+        quantise_half("q", 0, 0)
         score_pass(0)
         score_pass(1)
-        quantise("q", 0, PIXELS, PIXELS)
+        quantise_half("q", 0, 1)
+        regroup("k", 1, 1, "gpsimd")
 
         before = {
-            3: [lambda: quantise("k", 1)],
-            7: [lambda: quantise("q", 1), lambda: quantise_x(4, 2)],
-            9: [lambda: quantise_x(6, 2)],
-            15: [lambda: quantise("k", 2)],
+            3: [lambda: regroup_x(5, "vector"), lambda: quantise("k", 1), lambda: regroup("q", 1, 1, "gpsimd")],
+            7: [lambda: quantise("q", 1), lambda: quantise_x(4), lambda: quantise_x(5)],
+            15: [lambda: quantise("k", 2), lambda: quantise_x(6), lambda: quantise_x(7)],
             23: [lambda: quantise("k", 3)],
-            26: [lambda: quantise("q", 2)],
-            40: [lambda: quantise("q", 3)],
+            28: [lambda: quantise("q", 2)],
+            33: [lambda: quantise("q", 3)],
         }
         after = {
-            0: [lambda: regroup_shared("q", 1), lambda: regroup_x_shared(4), lambda: regroup_x_shared(6)],
-            7: [lambda: project("k", 2, range(4)), lambda: regroup_shared("k", 2)],
-            12: [lambda: project("k", 3, range(4)), lambda: regroup_shared("k", 3)],
-            16: [lambda: project("q", 2, range(4)), lambda: regroup_shared("q", 2)],
-            20: [lambda: project("q", 3, range(4)), lambda: regroup_shared("q", 3)],
+            0: [lambda: regroup("q", 1, 0, "scalar"), lambda: regroup_x(4, "scalar"), lambda: regroup_x(6, "scalar")],
+            7: [lambda: project("k", 2, range(4)), lambda: regroup_shared("k", 2), lambda: regroup_x(7, "scalar")],
+            15: [lambda: project("k", 3, range(4)), lambda: regroup_shared("k", 3)],
+            20: [lambda: project("q", 2, range(4)), lambda: regroup("q", 2, 0, "scalar")],
+            23: [lambda: regroup("q", 2, 1, "gpsimd")],
+            24: [lambda: project("q", 3, range(4)), lambda: regroup("q", 3, 0, "scalar")],
+            28: [lambda: regroup("q", 3, 1, "gpsimd")],
         }
         issued = 2
         for n in range(len(units) + GATE_LAG + 1):

@@ -27,7 +27,7 @@ GATE_SCALE = 1.0 / (IMAGES * math.sqrt(CHANNELS))
 
 EARLY_CHUNKS = 2 * CHUNKS_PER_PAIR
 LEAD = 3
-EARLY_DELAY = 5
+EARLY_DELAY = 1
 SPREAD_LAG = 1
 EXP_LAG = 3
 GATE_LAG = 5
@@ -39,8 +39,14 @@ STAGES = (
     (range(4), (1,)),
     (range(4, 8), (0, 1)),
     (range(8), (2,)),
+    (range(8, 12), (0,)),
+    (range(8, 10), (1,)),
     (range(8), (3,)),
-) + tuple(((chunk,), range(PAIRS)) for chunk in range(8, CHUNKS))
+    ((8,), (2, 3)),
+    ((9,), (2, 3)),
+    ((10,), (1, 2, 3)),
+    ((11,), (1, 2, 3)),
+) + tuple(((chunk,), range(PAIRS)) for chunk in range(12, CHUNKS))
 
 FLOPS = 2 * 2 * ALL_PIXELS * CHANNELS * CHANNELS + 2 * ALL_PIXELS * ALL_PIXELS * CHANNELS
 
@@ -65,12 +71,16 @@ def tile_coattlayer_pa_kernel(tc, x, Wq, bq, Wk, bk, out):
         bq_raw = keep.tile([P, PACK], BF16)
         nc.scalar.dma_start(out=bk_raw[:], in_=bk.rearrange("(p t) -> p t", t=PACK))
         nc.scalar.dma_start(out=bq_raw[:], in_=bq.rearrange("(p t) -> p t", t=PACK))
-        nc.sync.dma_start(out=wk_rows[:], in_=Wk.rearrange("(p t) c -> p (t c)", t=PACK))
-        for image in range(2):
-            nc.sync.dma_start(out=x_sb[:, image : image + 1], in_=x_view[:, image : image + 1])
-        nc.sync.dma_start(out=wq_rows[:], in_=Wq.rearrange("(p t) c -> p (t c)", t=PACK))
-        for pair in range(1, PAIRS):
-            nc.sync.dma_start(out=x_sb[:, 2 * pair : 2 * pair + 2], in_=x_view[:, 2 * pair : 2 * pair + 2])
+        nc.sync.dma_start(out=wk_rows[:, 0:1024], in_=Wk.rearrange("(p t) c -> p (t c)", t=PACK)[:, 0:1024])
+        nc.sync.dma_start(out=x_sb[:, 0:1], in_=x_view[:, 0:1])
+        nc.sync.dma_start(out=wk_rows[:, 1024:2048], in_=Wk.rearrange("(p t) c -> p (t c)", t=PACK)[:, 1024:2048])
+        nc.sync.dma_start(out=x_sb[:, 1:2], in_=x_view[:, 1:2])
+        nc.sync.dma_start(out=wq_rows[:, 0:1024], in_=Wq.rearrange("(p t) c -> p (t c)", t=PACK)[:, 0:1024])
+        nc.sync.dma_start(out=x_sb[:, 2:3], in_=x_view[:, 2:3])
+        nc.sync.dma_start(out=wq_rows[:, 1024:2048], in_=Wq.rearrange("(p t) c -> p (t c)", t=PACK)[:, 1024:2048])
+        nc.sync.dma_start(out=x_sb[:, 3:4], in_=x_view[:, 3:4])
+        nc.sync.dma_start(out=x_sb[:, 4:6], in_=x_view[:, 4:6])
+        nc.sync.dma_start(out=x_sb[:, 6:8], in_=x_view[:, 6:8])
 
         ident = keep.tile([P, P], F32)
         make_identity(nc, ident[:])
@@ -362,7 +372,6 @@ def tile_coattlayer_pa_kernel(tc, x, Wq, bq, Wk, bk, out):
         regroup("q", 0, 0, "vector")
         regroup("q", 0, 1, "vector")
         regroup("k", 1, 0, "scalar")
-        project("q", 1, range(4))
         quantise_half("q", 0, 0)
         score_pass(0)
         score_pass(1)
@@ -372,19 +381,22 @@ def tile_coattlayer_pa_kernel(tc, x, Wq, bq, Wk, bk, out):
         before = {
             3: [lambda: regroup_x(5, "vector"), lambda: quantise("k", 1), lambda: regroup("q", 1, 1, "gpsimd")],
             7: [lambda: quantise("q", 1), lambda: quantise_x(4), lambda: quantise_x(5)],
-            15: [lambda: quantise("k", 2), lambda: quantise_x(6), lambda: quantise_x(7)],
-            23: [lambda: quantise("k", 3)],
-            28: [lambda: quantise("q", 2)],
-            33: [lambda: quantise("q", 3)],
+            15: [lambda: quantise("k", 2), lambda: regroup("q", 2, 1, "gpsimd")],
+            17: [lambda: quantise_x(6), lambda: quantise_x(7)],
+            23: [lambda: quantise("q", 2)],
+            29: [lambda: quantise("k", 3), lambda: regroup("q", 3, 1, "gpsimd")],
+            35: [lambda: quantise("q", 3)],
         }
         after = {
-            0: [lambda: regroup("q", 1, 0, "scalar"), lambda: regroup_x(4, "scalar"), lambda: regroup_x(6, "scalar")],
-            7: [lambda: project("k", 2, range(4)), lambda: regroup_shared("k", 2), lambda: regroup_x(7, "scalar")],
-            15: [lambda: project("k", 3, range(4)), lambda: regroup_shared("k", 3)],
-            20: [lambda: project("q", 2, range(4)), lambda: regroup("q", 2, 0, "scalar")],
-            23: [lambda: regroup("q", 2, 1, "gpsimd")],
-            24: [lambda: project("q", 3, range(4)), lambda: regroup("q", 3, 0, "scalar")],
-            28: [lambda: regroup("q", 3, 1, "gpsimd")],
+            0: [lambda: project("q", 1, range(4)), lambda: regroup("q", 1, 0, "scalar"), lambda: regroup_x(4, "scalar"), lambda: regroup_x(6, "scalar")],
+            7: [lambda: project("k", 2, (0, 1))],
+            8: [lambda: project("k", 2, (2, 3)), lambda: regroup_shared("k", 2), lambda: regroup_x(7, "scalar")],
+            9: [lambda: project("q", 2, (0, 1))],
+            10: [lambda: project("q", 2, (2, 3)), lambda: regroup("q", 2, 0, "scalar")],
+            17: [lambda: project("k", 3, (0, 1))],
+            18: [lambda: project("k", 3, (2, 3)), lambda: regroup("k", 3, 0, "scalar")],
+            23: [lambda: regroup("k", 3, 1, "gpsimd"), lambda: project("q", 3, (0, 1))],
+            24: [lambda: project("q", 3, (2, 3)), lambda: regroup("q", 3, 0, "scalar")],
         }
         issued = 2
         for n in range(len(units) + GATE_LAG + 1):

@@ -89,6 +89,14 @@ def tile_coattlayer_pa_kernel(tc, x, Wq, bq, Wk, bk, out):
         nc.gpsimd.tensor_copy(out=bk_f32[:], in_=bk_raw[:])
         nc.gpsimd.tensor_copy(out=bq_f32[:], in_=bq_raw[:])
 
+        zeros = keep.tile([P, PAIR], BF16)
+        nc.vector.memset(zeros[:], 0)
+
+        def warm_up(passes):
+            for turn in range(passes):
+                idle = psum_proj.tile([P, PAIR], F32, tag="proj")
+                nc.tensor.matmul(out=idle[:], lhsT=zeros[:, 0:P], rhs=zeros[:], start=True, stop=True)
+
         x_codes = keep.tile([P, ALL_PIXELS], U32, align_bytes=64)
         x_scales = keep.tile([P, ALL_PIXELS], U8, align_bytes=64)
         wk_codes = keep.tile([P, CHANNELS], U32, align_bytes=64)
@@ -344,8 +352,11 @@ def tile_coattlayer_pa_kernel(tc, x, Wq, bq, Wk, bk, out):
 
         wk_grouped = new_w_grouped()
         wq_grouped = new_w_grouped()
+        warm_up(5)
         turn_half(wk_rows, wk_grouped, 0, on_vector=False)
+        warm_up(2)
         turn_half(wk_rows, wk_grouped, 1, on_vector=False)
+        warm_up(2)
         regroup_x(0, "vector")
         regroup_x(1, "vector")
         quantise_x(0)
@@ -353,6 +364,7 @@ def tile_coattlayer_pa_kernel(tc, x, Wq, bq, Wk, bk, out):
         quantise_w_half(sides["k"], wk_grouped, 0)
         quantise_w_half(sides["k"], wk_grouped, 1)
         turn_half(wq_rows, wq_grouped, 0, on_vector=False)
+        warm_up(2)
         turn_half(wq_rows, wq_grouped, 1, on_vector=False)
         project("k", 0, range(3))
         regroup_x(2, "vector")

@@ -358,22 +358,23 @@ def tile_coattlayer_pa_kernel(tc, x, Wq, bq, Wk, bk, out):
         turn_half(wk_rows, wk_grouped, 1, on_vector=False)
         warm_up(2)
         regroup_x(0, "vector")
-        regroup_x(1, "vector")
         quantise_x(0)
-        quantise_x(1)
+        regroup_x(1, "vector")
         quantise_w_half(sides["k"], wk_grouped, 0)
+        quantise_x(1)
         quantise_w_half(sides["k"], wk_grouped, 1)
         turn_half(wq_rows, wq_grouped, 0, on_vector=False)
-        warm_up(2)
+        warm_up(1)
+        project("k", 0, (0,))
         turn_half(wq_rows, wq_grouped, 1, on_vector=False)
-        project("k", 0, range(3))
+        project("k", 0, (1, 2, 3))
         regroup_x(2, "vector")
         regroup_x(3, "vector")
         quantise_w_half(sides["q"], wq_grouped, 0)
-        quantise_w_half(sides["q"], wq_grouped, 1)
         quantise_x(2)
         quantise_x(3)
-        project("k", 0, (3,), on_vector=True)
+        quantise_w_half(sides["q"], wq_grouped, 1)
+        regroup_x(5, "vector")
         project("q", 0, (3,), on_vector=True)
         project("q", 0, range(3))
         regroup("k", 0, 0, "vector")
@@ -389,10 +390,11 @@ def tile_coattlayer_pa_kernel(tc, x, Wq, bq, Wk, bk, out):
         score_pass(1)
         quantise_half("q", 0, 1)
         regroup("k", 1, 1, "gpsimd")
+        regroup_x(4, "vector")
 
         before = {
-            3: [lambda: regroup_x(5, "vector"), lambda: quantise("k", 1), lambda: regroup("q", 1, 1, "gpsimd")],
-            7: [lambda: quantise("q", 1), lambda: quantise_x(4), lambda: quantise_x(5)],
+            3: [lambda: quantise("k", 1), lambda: quantise_x(4), lambda: quantise_x(5), lambda: regroup("q", 1, 1, "gpsimd")],
+            7: [lambda: quantise("q", 1)],
             15: [lambda: quantise("k", 2), lambda: regroup("q", 2, 1, "gpsimd")],
             17: [lambda: quantise_x(6), lambda: quantise_x(7)],
             23: [lambda: quantise("q", 2)],
@@ -400,9 +402,10 @@ def tile_coattlayer_pa_kernel(tc, x, Wq, bq, Wk, bk, out):
             35: [lambda: quantise("q", 3)],
         }
         after = {
-            0: [lambda: project("q", 1, range(4)), lambda: regroup("q", 1, 0, "scalar"), lambda: regroup_x(4, "scalar"), lambda: regroup_x(6, "scalar")],
-            7: [lambda: project("k", 2, (0, 1))],
-            8: [lambda: project("k", 2, (2, 3)), lambda: regroup_shared("k", 2), lambda: regroup_x(7, "scalar")],
+            0: [lambda: project("q", 1, range(4)), lambda: regroup("q", 1, 0, "scalar")],
+            3: [lambda: project("k", 2, (0, 1))],
+            4: [lambda: project("k", 2, (2, 3)), lambda: regroup("k", 2, 0, "scalar"), lambda: regroup_x(6, "scalar"), lambda: regroup_x(7, "scalar")],
+            7: [lambda: regroup("k", 2, 1, "gpsimd")],
             9: [lambda: project("q", 2, (0, 1))],
             10: [lambda: project("q", 2, (2, 3)), lambda: regroup("q", 2, 0, "scalar")],
             17: [lambda: project("k", 3, (0, 1))],

@@ -395,10 +395,10 @@ def tile_coattlayer_pa_kernel(tc, x, Wq, bq, Wk, bk, out):
         before = {
             3: [lambda: quantise("k", 1), lambda: quantise_x(4), lambda: quantise_x(5), lambda: regroup("q", 1, 1, "gpsimd")],
             7: [lambda: quantise("q", 1)],
-            15: [lambda: quantise("k", 2), lambda: regroup("q", 2, 1, "gpsimd")],
+            14: [lambda: quantise("k", 2), lambda: regroup("q", 2, 1, "gpsimd")],
             17: [lambda: quantise_x(6), lambda: quantise_x(7)],
             23: [lambda: quantise("q", 2)],
-            29: [lambda: quantise("k", 3), lambda: regroup("q", 3, 1, "gpsimd")],
+            28: [lambda: quantise("k", 3), lambda: regroup("q", 3, 1, "gpsimd")],
             35: [lambda: quantise("q", 3)],
         }
         after = {

@@ -27,8 +27,9 @@ GATE_SCALE = 1.0 / (IMAGES * math.sqrt(CHANNELS))
 
 EARLY_CHUNKS = 2 * CHUNKS_PER_PAIR
 LEAD = 3
-EARLY_DELAY = 1
+EARLY_DELAY = 0
 SPREAD_LAG = 1
+VECTOR_ROW = 1
 EXP_LAG = 3
 GATE_LAG = 5
 QUANT_FIRST = 10
@@ -40,11 +41,11 @@ STAGES = (
     (range(4, 8), (0, 1)),
     (range(8), (2,)),
     (range(8, 12), (0,)),
-    (range(8, 10), (1,)),
+    (range(8, 11), (1,)),
     (range(8), (3,)),
     ((8,), (2, 3)),
     ((9,), (2, 3)),
-    ((10,), (1, 2, 3)),
+    ((10,), (2, 3)),
     ((11,), (1, 2, 3)),
 ) + tuple(((chunk,), range(PAIRS)) for chunk in range(12, CHUNKS))
 
@@ -266,9 +267,12 @@ def tile_coattlayer_pa_kernel(tc, x, Wq, bq, Wk, bk, out):
             )
 
         totals = {}
+        lowers = {}
         spreads = {}
         numers = {}
         denoms = {}
+        inverses = {}
+        products = {}
 
         def add_up(image):
             total = small.tile([P, 2], F32, tag="total")
@@ -282,25 +286,39 @@ def tile_coattlayer_pa_kernel(tc, x, Wq, bq, Wk, bk, out):
                     accum_out=total[:, h : h + 1],
                 )
             totals[image] = total
+            if image < IMAGES - 1:
+                excess = small.tile([P, 1], F32, tag="excess")
+                nc.scalar.activation(
+                    out=excess[:], in_=total[:, 0:1], func=ACT.Relu, bias=total[:, 1:2], scale=-1.0
+                )
+                lower = small.tile([P, 1], F32, tag="lower")
+                nc.scalar.activation(
+                    out=lower[:], in_=excess[:], func=ACT.Identity, bias=total[:, 1:2], scale=-1.0
+                )
+                lowers[image] = lower
 
         def spread_out(image):
-            spread = psum_proj.tile([P, PIXELS], F32, tag="proj")
-            for h in range(2):
+            spread = psum_proj.tile([P, PIXELS + P], F32, tag="proj")
+            columns = [totals[image][:, 0:1], totals[image][:, 1:2]]
+            if image < IMAGES - 1:
+                columns += [lowers[image][:]]
+            for h, column in enumerate(columns):
                 nc.tensor.transpose(
                     out=spread[:, h * P : (h + 1) * P],
-                    in_=totals[image][:, h : h + 1].to_broadcast([P, P]),
+                    in_=column.to_broadcast([P, P]),
                     identity=ident[:],
                 )
             spreads[image] = spread
 
         def exponentials(image):
             shift = small.tile([P, 1], F32, tag="shift")
-            nc.vector.tensor_reduce(out=shift[:], in_=spreads[image][:], axis=AXIS_X, op=ALU.min)
+            sources = slice(PIXELS, PIXELS + P) if image < IMAGES - 1 else slice(0, PIXELS)
+            nc.vector.tensor_reduce(out=shift[:], in_=spreads[image][:, sources], axis=AXIS_X, op=ALU.min)
             numer = small.tile([P, PIXELS], F32, tag="numer")
             denom = small.tile([P, 1], F32, tag="denom")
             nc.scalar.activation(
                 out=numer[:],
-                in_=spreads[image][:],
+                in_=spreads[image][:, 0:PIXELS],
                 func=ACT.Exp,
                 bias=shift[:, 0:1],
                 scale=-1.0,
@@ -309,34 +327,48 @@ def tile_coattlayer_pa_kernel(tc, x, Wq, bq, Wk, bk, out):
             numers[image] = numer
             denoms[image] = denom
 
+        def multiply_on_vector(image, row):
+            nc.vector.scalar_tensor_tensor(
+                out=products[image][:, row, :],
+                in0=x_sb[:, image, row, :],
+                scalar=inverses[image][:, 0:1],
+                in1=numers[image][:],
+                op0=ALU.mult,
+                op1=ALU.mult,
+            )
+
         def gate_and_store(image):
             inverse = small.tile([P, 1], F32, tag="inverse")
             nc.vector.reciprocal(out=inverse[:], in_=denoms[image][:])
+            inverses[image] = inverse
             product = results.tile([P, PACK, PIXELS], F32, tag="product")
-            if image < IMAGES - 1:
-                gate = small.tile([P, PIXELS], F32, tag="gate")
-                nc.scalar.activation(out=gate[:], in_=numers[image][:], func=ACT.Copy, scale=inverse[:, 0:1])
-                nc.gpsimd.tensor_tensor(
-                    out=product[:],
-                    in0=x_sb[:, image],
-                    in1=gate[:].unsqueeze(1).to_broadcast([P, PACK, PIXELS]),
-                    op=ALU.mult,
-                )
-                nc.sync.dma_start(out=out_view[image], in_=product[:])
-            else:
-                for j in range(PACK):
-                    rows = slice(j, j + 1)
-                    nc.vector.scalar_tensor_tensor(
-                        out=product[:, rows, :],
-                        in0=x_sb[:, image, rows, :],
-                        scalar=inverse[:, 0:1],
-                        in1=numers[image][:].unsqueeze(1).to_broadcast([P, 1, PIXELS]),
-                        op0=ALU.mult,
-                        op1=ALU.mult,
-                    )
-                    nc.sync.dma_start(out=out_view[image][:, rows, :], in_=product[:, rows, :])
+            products[image] = product
+            if image == IMAGES - 1:
+                for row in range(PACK):
+                    multiply_on_vector(image, row)
+                    nc.sync.dma_start(out=out_view[image][:, row, :], in_=product[:, row, :])
+                return
+            rows = slice(0, VECTOR_ROW if image == IMAGES - 2 else PACK)
+            gate = small.tile([P, PIXELS], F32, tag="gate")
+            nc.scalar.activation(out=gate[:], in_=numers[image][:], func=ACT.Copy, scale=inverse[:, 0:1])
+            nc.gpsimd.tensor_tensor(
+                out=product[:, rows, :],
+                in0=x_sb[:, image, rows, :],
+                in1=gate[:].unsqueeze(1).to_broadcast([P, rows.stop, PIXELS]),
+                op=ALU.mult,
+            )
+            nc.sync.dma_start(out=out_view[image][:, rows, :], in_=product[:, rows, :])
+
+        def multiply_the_rest():
+            image = IMAGES - 2
+            for row in range(VECTOR_ROW, PACK):
+                multiply_on_vector(image, row)
+            rows = slice(VECTOR_ROW, PACK)
+            nc.sync.dma_start(out=out_view[image][:, rows, :], in_=products[image][:, rows, :])
 
         def endings(n):
+            if n == len(units):
+                multiply_the_rest()
             for image in range(IMAGES):
                 last_unit = max(units.index((2 * image + h, pair)) for h in range(2) for pair in range(PAIRS))
                 if 2 * image < EARLY_CHUNKS:
@@ -397,9 +429,9 @@ def tile_coattlayer_pa_kernel(tc, x, Wq, bq, Wk, bk, out):
             7: [lambda: quantise("q", 1)],
             14: [lambda: quantise("k", 2), lambda: regroup("q", 2, 1, "gpsimd")],
             17: [lambda: quantise_x(6), lambda: quantise_x(7)],
-            23: [lambda: quantise("q", 2)],
-            28: [lambda: quantise("k", 3), lambda: regroup("q", 3, 1, "gpsimd")],
-            35: [lambda: quantise("q", 3)],
+            22: [lambda: quantise("q", 2)],
+            29: [lambda: quantise("k", 3), lambda: regroup("q", 3, 1, "gpsimd")],
+            36: [lambda: quantise("q", 3)],
         }
         after = {
             0: [lambda: project("q", 1, range(4)), lambda: regroup("q", 1, 0, "scalar")],
@@ -410,7 +442,8 @@ def tile_coattlayer_pa_kernel(tc, x, Wq, bq, Wk, bk, out):
             10: [lambda: project("q", 2, (2, 3)), lambda: regroup("q", 2, 0, "scalar")],
             17: [lambda: project("k", 3, (0, 1))],
             18: [lambda: project("k", 3, (2, 3)), lambda: regroup("k", 3, 0, "scalar")],
-            23: [lambda: regroup("k", 3, 1, "gpsimd"), lambda: project("q", 3, (0, 1))],
+            22: [lambda: regroup("k", 3, 1, "gpsimd")],
+            23: [lambda: project("q", 3, (0, 1))],
             24: [lambda: project("q", 3, (2, 3)), lambda: regroup("q", 3, 0, "scalar")],
         }
         issued = 2

@@ -29,9 +29,8 @@ EARLY_CHUNKS = 2 * CHUNKS_PER_PAIR
 LEAD = 3
 EARLY_DELAY = 0
 SPREAD_LAG = 1
-VECTOR_ROW = 1
-EXP_LAG = 3
-GATE_LAG = 5
+EXP_LAG = 4
+GATE_LAG = 6
 QUANT_FIRST = 10
 QUANT_EVERY = 7
 
@@ -41,11 +40,11 @@ STAGES = (
     (range(4, 8), (0, 1)),
     (range(8), (2,)),
     (range(8, 12), (0,)),
-    (range(8, 11), (1,)),
+    (range(8, 10), (1,)),
     (range(8), (3,)),
     ((8,), (2, 3)),
     ((9,), (2, 3)),
-    ((10,), (2, 3)),
+    ((10,), (1, 2, 3)),
     ((11,), (1, 2, 3)),
 ) + tuple(((chunk,), range(PAIRS)) for chunk in range(12, CHUNKS))
 
@@ -348,27 +347,30 @@ def tile_coattlayer_pa_kernel(tc, x, Wq, bq, Wk, bk, out):
                     multiply_on_vector(image, row)
                     nc.sync.dma_start(out=out_view[image][:, row, :], in_=product[:, row, :])
                 return
-            rows = slice(0, VECTOR_ROW if image == IMAGES - 2 else PACK)
+            if image == IMAGES - 2:
+                return
             gate = small.tile([P, PIXELS], F32, tag="gate")
             nc.scalar.activation(out=gate[:], in_=numers[image][:], func=ACT.Copy, scale=inverse[:, 0:1])
             nc.gpsimd.tensor_tensor(
-                out=product[:, rows, :],
-                in0=x_sb[:, image, rows, :],
-                in1=gate[:].unsqueeze(1).to_broadcast([P, rows.stop, PIXELS]),
+                out=product[:],
+                in0=x_sb[:, image],
+                in1=gate[:].unsqueeze(1).to_broadcast([P, PACK, PIXELS]),
                 op=ALU.mult,
             )
-            nc.sync.dma_start(out=out_view[image][:, rows, :], in_=product[:, rows, :])
+            nc.sync.dma_start(out=out_view[image], in_=product[:])
 
-        def multiply_the_rest():
+        def multiply_second_last(first, count):
             image = IMAGES - 2
-            for row in range(VECTOR_ROW, PACK):
+            for row in range(first, first + count):
                 multiply_on_vector(image, row)
-            rows = slice(VECTOR_ROW, PACK)
+            rows = slice(first, first + count)
             nc.sync.dma_start(out=out_view[image][:, rows, :], in_=products[image][:, rows, :])
 
         def endings(n):
             if n == len(units):
-                multiply_the_rest()
+                multiply_second_last(0, 3)
+            if n == len(units) + EXP_LAG:
+                multiply_second_last(3, 1)
             for image in range(IMAGES):
                 last_unit = max(units.index((2 * image + h, pair)) for h in range(2) for pair in range(PAIRS))
                 if 2 * image < EARLY_CHUNKS:
@@ -386,9 +388,9 @@ def tile_coattlayer_pa_kernel(tc, x, Wq, bq, Wk, bk, out):
         wq_grouped = new_w_grouped()
         warm_up(5)
         turn_half(wk_rows, wk_grouped, 0, on_vector=False)
-        warm_up(2)
+        warm_up(1)
         turn_half(wk_rows, wk_grouped, 1, on_vector=False)
-        warm_up(2)
+        warm_up(1)
         regroup_x(0, "vector")
         quantise_x(0)
         regroup_x(1, "vector")
@@ -412,6 +414,7 @@ def tile_coattlayer_pa_kernel(tc, x, Wq, bq, Wk, bk, out):
         regroup("k", 0, 0, "vector")
         regroup("k", 0, 1, "vector")
         project("k", 1, range(4))
+        warm_up(2)
         quantise_half("k", 0, 0)
         quantise_half("k", 0, 1)
         regroup("q", 0, 0, "vector")
@@ -430,8 +433,8 @@ def tile_coattlayer_pa_kernel(tc, x, Wq, bq, Wk, bk, out):
             14: [lambda: quantise("k", 2), lambda: regroup("q", 2, 1, "gpsimd")],
             17: [lambda: quantise_x(6), lambda: quantise_x(7)],
             22: [lambda: quantise("q", 2)],
-            29: [lambda: quantise("k", 3), lambda: regroup("q", 3, 1, "gpsimd")],
-            36: [lambda: quantise("q", 3)],
+            28: [lambda: quantise("k", 3), lambda: regroup("q", 3, 1, "gpsimd")],
+            35: [lambda: quantise("q", 3)],
         }
         after = {
             0: [lambda: project("q", 1, range(4)), lambda: regroup("q", 1, 0, "scalar")],

@@ -40,11 +40,11 @@ STAGES = (
     (range(4, 8), (0, 1)),
     (range(8), (2,)),
     (range(8, 12), (0,)),
-    (range(8, 10), (1,)),
+    (range(8, 11), (1,)),
     (range(8), (3,)),
     ((8,), (2, 3)),
     ((9,), (2, 3)),
-    ((10,), (1, 2, 3)),
+    ((10,), (2, 3)),
     ((11,), (1, 2, 3)),
 ) + tuple(((chunk,), range(PAIRS)) for chunk in range(12, CHUNKS))
 
@@ -433,8 +433,8 @@ def tile_coattlayer_pa_kernel(tc, x, Wq, bq, Wk, bk, out):
             14: [lambda: quantise("k", 2), lambda: regroup("q", 2, 1, "gpsimd")],
             17: [lambda: quantise_x(6), lambda: quantise_x(7)],
             22: [lambda: quantise("q", 2)],
-            28: [lambda: quantise("k", 3), lambda: regroup("q", 3, 1, "gpsimd")],
-            35: [lambda: quantise("q", 3)],
+            29: [lambda: quantise("k", 3), lambda: regroup("q", 3, 1, "gpsimd")],
+            36: [lambda: quantise("q", 3)],
         }
         after = {
             0: [lambda: project("q", 1, range(4)), lambda: regroup("q", 1, 0, "scalar")],

import math
from contextlib import ExitStack

import concourse.mybir as mybir
from concourse.masks import make_identity

BF16 = mybir.dt.bfloat16
F32 = mybir.dt.float32
U32 = mybir.dt.uint32
U8 = mybir.dt.uint8
FP8X4 = mybir.dt.float8_e4m3fn_x4
ALU = mybir.AluOpType
ACT = mybir.ActivationFunctionType
AXIS_X = mybir.AxisListType.X

P = 128
PACK = 4
IMAGES = 8
CHANNELS = P * PACK
PIXELS = 256
PAIR = 2 * PIXELS
PAIRS = IMAGES // 2
ALL_PIXELS = IMAGES * PIXELS
CHUNKS = ALL_PIXELS // P
CHUNKS_PER_PAIR = PAIR // P
GATE_SCALE = 1.0 / (IMAGES * math.sqrt(CHANNELS))

EARLY_CHUNKS = 2 * CHUNKS_PER_PAIR
LEAD = 3
EARLY_DELAY = 0
SPREAD_LAG = 1
EXP_LAG = 4
GATE_LAG = 6
QUANT_FIRST = 10
QUANT_EVERY = 7

STAGES = (
    (range(4), (0,)),
    (range(4), (1,)),
    (range(4, 8), (0, 1)),
    (range(8), (2,)),
    (range(8, 12), (0,)),
    (range(8, 11), (1,)),
    (range(8), (3,)),
    ((8,), (2, 3)),
    ((9,), (2, 3)),
    ((10,), (2, 3)),
    ((11,), (1, 2, 3)),
) + tuple(((chunk,), range(PAIRS)) for chunk in range(12, CHUNKS))

FLOPS = 2 * 2 * ALL_PIXELS * CHANNELS * CHANNELS + 2 * ALL_PIXELS * ALL_PIXELS * CHANNELS


def tile_coattlayer_pa_kernel(tc, x, Wq, bq, Wk, bk, out):
    nc = tc.nc
    with ExitStack() as stack:
        keep = stack.enter_context(tc.tile_pool(name="keep", bufs=1))
        stage = stack.enter_context(tc.tile_pool(name="stage", bufs=2))
        small = stack.enter_context(tc.tile_pool(name="small", bufs=4))
        results = stack.enter_context(tc.tile_pool(name="results", bufs=4))
        psum_proj = stack.enter_context(tc.psum_pool(name="psum_proj", bufs=4))
        psum_score = stack.enter_context(tc.psum_pool(name="psum_score", bufs=4))
        stack.enter_context(tc.manual_schedule())

        x_view = x.rearrange("b (p j) h w -> p b j (h w)", j=PACK)
        out_view = out.rearrange("b (p j) h w -> b p j (h w)", j=PACK)
        x_sb = keep.tile([P, IMAGES, PACK, PIXELS], BF16)
        wk_rows = keep.tile([P, PACK * CHANNELS], BF16)
        wq_rows = keep.tile([P, PACK * CHANNELS], BF16)
        bk_raw = keep.tile([P, PACK], BF16)
        bq_raw = keep.tile([P, PACK], BF16)
        nc.scalar.dma_start(out=bk_raw[:], in_=bk.rearrange("(p t) -> p t", t=PACK))
        nc.scalar.dma_start(out=bq_raw[:], in_=bq.rearrange("(p t) -> p t", t=PACK))
        nc.sync.dma_start(out=wk_rows[:, 0:1024], in_=Wk.rearrange("(p t) c -> p (t c)", t=PACK)[:, 0:1024])
        nc.sync.dma_start(out=x_sb[:, 0:1], in_=x_view[:, 0:1])
        nc.sync.dma_start(out=wk_rows[:, 1024:2048], in_=Wk.rearrange("(p t) c -> p (t c)", t=PACK)[:, 1024:2048])
        nc.sync.dma_start(out=x_sb[:, 1:2], in_=x_view[:, 1:2])
        nc.sync.dma_start(out=wq_rows[:, 0:1024], in_=Wq.rearrange("(p t) c -> p (t c)", t=PACK)[:, 0:1024])
        nc.sync.dma_start(out=x_sb[:, 2:3], in_=x_view[:, 2:3])
        nc.sync.dma_start(out=wq_rows[:, 1024:2048], in_=Wq.rearrange("(p t) c -> p (t c)", t=PACK)[:, 1024:2048])
        nc.sync.dma_start(out=x_sb[:, 3:4], in_=x_view[:, 3:4])
        nc.sync.dma_start(out=x_sb[:, 4:6], in_=x_view[:, 4:6])
        nc.sync.dma_start(out=x_sb[:, 6:8], in_=x_view[:, 6:8])

        ident = keep.tile([P, P], F32)
        make_identity(nc, ident[:])
        bk_f32 = keep.tile([P, PACK], F32)
        bq_f32 = keep.tile([P, PACK], F32)
        nc.gpsimd.tensor_copy(out=bk_f32[:], in_=bk_raw[:])
        nc.gpsimd.tensor_copy(out=bq_f32[:], in_=bq_raw[:])

        zeros = keep.tile([P, PAIR], BF16)
        nc.vector.memset(zeros[:], 0)

        def warm_up(passes):
            for turn in range(passes):
                idle = psum_proj.tile([P, PAIR], F32, tag="proj")
                nc.tensor.matmul(out=idle[:], lhsT=zeros[:, 0:P], rhs=zeros[:], start=True, stop=True)

        x_codes = keep.tile([P, ALL_PIXELS], U32, align_bytes=64)
        x_scales = keep.tile([P, ALL_PIXELS], U8, align_bytes=64)
        wk_codes = keep.tile([P, CHANNELS], U32, align_bytes=64)
        wk_scales = keep.tile([P, CHANNELS], U8, align_bytes=64)
        wq_codes = keep.tile([P, CHANNELS], U32, align_bytes=64)
        wq_scales = keep.tile([P, CHANNELS], U8, align_bytes=64)
        k_codes = keep.tile([P, ALL_PIXELS], U32, align_bytes=64)
        k_scales = keep.tile([P, ALL_PIXELS], U8, align_bytes=64)
        q_codes = keep.tile([P, ALL_PIXELS], U32, align_bytes=64)
        q_scales = keep.tile([P, ALL_PIXELS], U8, align_bytes=64)
        best = keep.tile([P, CHUNKS, IMAGES], F32)
        sides = {}
        sides["k"] = {"w_codes": wk_codes, "w_scales": wk_scales, "bias": bk_f32, "codes": k_codes, "scales": k_scales}
        sides["q"] = {"w_codes": wq_codes, "w_scales": wq_scales, "bias": bq_f32, "codes": q_codes, "scales": q_scales}

        def pair_cols(pair):
            return slice(pair * PAIR, (pair + 1) * PAIR)

        def turn_half(rows, grouped, half, on_vector):
            words = rows[:].bitcast(F32).rearrange("p (t q u) -> p t u q", t=PACK, u=2)
            grouped_words = grouped[:].bitcast(F32).rearrange("p (t d u) -> p t d u", t=PACK, u=2)
            turned = psum_score.tile([P, 2, 2, P], F32, tag="score")
            for a in range(2):
                for u in range(2):
                    nc.tensor.transpose(out=turned[:, a, u, :], in_=words[:, 2 * half + a, u, :], identity=ident[:])
            target = grouped_words[:, 2 * half : 2 * half + 2]
            source = turned[:].rearrange("p a u d -> p a d u")
            if on_vector:
                nc.vector.tensor_copy(out=target, in_=source)
            else:
                nc.scalar.copy(out=target, in_=source)

        def quantise_w_half(side, grouped, half):
            cols = slice(half * 2 * P, (half + 1) * 2 * P)
            nc.vector.quantize_mx(
                out=side["w_codes"][:, cols].bitcast(FP8X4),
                scales=side["w_scales"][:, cols],
                in_=grouped[:, half * 2 * P * PACK : (half + 1) * 2 * P * PACK],
            )

        def new_w_grouped():
            grouped = stage.tile([P, PACK * CHANNELS], BF16, tag="w_grouped", align_bytes=64)
            return grouped

        x_grouped = {}

        def interleave(engine, grouped, rows):
            if engine == "gpsimd":
                nc.gpsimd.tensor_scalar(
                    out=grouped,
                    in0=rows.rearrange("p j n -> p n j"),
                    scalar1=1.0,
                    scalar2=0.0,
                    op0=ALU.mult,
                    op1=ALU.add,
                )
                return
            target = grouped.rearrange("p (c r) j -> p c j r", r=4)
            source = rows.rearrange("p j (c r) -> p c j r", r=4)
            if engine == "scalar":
                nc.scalar.copy(out=target, in_=source)
            else:
                nc.vector.tensor_copy(out=target, in_=source)

        def regroup_x(image, engine):
            grouped = stage.tile([P, PIXELS, PACK], BF16, tag="x_grouped", bufs=IMAGES, align_bytes=64)
            interleave(engine, grouped[:], x_sb[:, image, :, :])
            x_grouped[image] = grouped

        def quantise_x(image):
            cols = slice(image * PIXELS, (image + 1) * PIXELS)
            nc.vector.quantize_mx(
                out=x_codes[:, cols].bitcast(FP8X4),
                scales=x_scales[:, cols],
                in_=x_grouped[image][:].rearrange("p w j -> p (w j)"),
            )

        def project_pass(side, pair, planes, t, on_vector):
            acc = psum_proj.tile([P, PAIR], F32, tag="proj")
            nc.tensor.matmul_mx(
                out=acc[:],
                lhsT=side["w_codes"][:, t * P : (t + 1) * P].bitcast(FP8X4),
                lhsT_scale=side["w_scales"][:, t * P : (t + 1) * P],
                rhs=x_codes[:, pair_cols(pair)].bitcast(FP8X4),
                rhs_scale=x_scales[:, pair_cols(pair)],
                start=True,
                stop=True,
            )
            bias = side["bias"][:, t : t + 1]
            if on_vector:
                nc.vector.tensor_scalar(
                    out=planes[:, t, :], in0=acc[:], scalar1=bias, scalar2=None, op0=ALU.add
                )
            else:
                nc.scalar.activation(out=planes[:, t, :], in_=acc[:], func=ACT.Identity, bias=bias, scale=1.0)

        all_planes = {}
        grouped_halves = {}

        def project(name, pair, passes, on_vector=False):
            for t in passes:
                if (name, pair) not in all_planes:
                    planes = stage.tile([P, PACK, PAIR], BF16, tag="planes", bufs=3)
                    all_planes[name, pair] = planes
                project_pass(sides[name], pair, all_planes[name, pair], t, on_vector)

        def regroup(name, pair, half, engine):
            if half == 0:
                grouped = stage.tile([P, PIXELS, PACK], BF16, tag="grouped_0", bufs=4, align_bytes=64)
            else:
                grouped = stage.tile([P, PIXELS, PACK], BF16, tag="grouped_1", bufs=1, align_bytes=64)
            cols = slice(half * PIXELS, (half + 1) * PIXELS)
            interleave(engine, grouped[:], all_planes[name, pair][:, :, cols])
            grouped_halves[name, pair, half] = grouped

        def regroup_shared(name, pair):
            regroup(name, pair, 0, "scalar")
            regroup(name, pair, 1, "gpsimd")

        def quantise_half(name, pair, half):
            side = sides[name]
            image = 2 * pair + half
            cols = slice(image * PIXELS, (image + 1) * PIXELS)
            nc.vector.quantize_mx(
                out=side["codes"][:, cols].bitcast(FP8X4),
                scales=side["scales"][:, cols],
                in_=grouped_halves[name, pair, half][:].rearrange("p n t -> p (n t)"),
            )
            ready.add((name, image))

        def quantise(name, pair):
            quantise_half(name, pair, 0)
            quantise_half(name, pair, 1)

        ready = set()

        units = []
        for chunks, pairs in STAGES:
            units += [(chunk, pair) for pair in pairs for chunk in chunks]
        banks = {}

        def available(n):
            chunk, pair = units[n]
            return ("q", chunk // 2) in ready and ("k", 2 * pair + 1) in ready

        def score_pass(n):
            chunk, pair = units[n]
            acc = psum_score.tile([P, PAIR], F32, tag="score")
            nc.tensor.matmul_mx(
                out=acc[:],
                lhsT=q_codes[:, chunk * P : (chunk + 1) * P].bitcast(FP8X4),
                lhsT_scale=q_scales[:, chunk * P : (chunk + 1) * P],
                rhs=k_codes[:, pair_cols(pair)].bitcast(FP8X4),
                rhs_scale=k_scales[:, pair_cols(pair)],
                start=True,
                stop=True,
            )
            banks[n] = acc

        def take_maxima(n):
            chunk, pair = units[n]
            nc.vector.tensor_reduce(
                out=best[:, chunk, 2 * pair : 2 * pair + 2],
                in_=banks[n][:].rearrange("p (i m) -> p i m", i=2),
                axis=AXIS_X,
                op=ALU.max,
            )

        totals = {}
        lowers = {}
        spreads = {}
        numers = {}
        denoms = {}
        inverses = {}
        products = {}

        def add_up(image):
            total = small.tile([P, 2], F32, tag="total")
            scaled = small.tile([P, 2, IMAGES], F32, tag="scaled")
            for h in range(2):
                nc.scalar.activation(
                    out=scaled[:, h, :],
                    in_=best[:, 2 * image + h, :],
                    func=ACT.Copy,
                    scale=-GATE_SCALE,
                    accum_out=total[:, h : h + 1],
                )
            totals[image] = total
            if image < IMAGES - 1:
                excess = small.tile([P, 1], F32, tag="excess")
                nc.scalar.activation(
                    out=excess[:], in_=total[:, 0:1], func=ACT.Relu, bias=total[:, 1:2], scale=-1.0
                )
                lower = small.tile([P, 1], F32, tag="lower")
                nc.scalar.activation(
                    out=lower[:], in_=excess[:], func=ACT.Identity, bias=total[:, 1:2], scale=-1.0
                )
                lowers[image] = lower

        def spread_out(image):
            spread = psum_proj.tile([P, PIXELS + P], F32, tag="proj")
            columns = [totals[image][:, 0:1], totals[image][:, 1:2]]
            if image < IMAGES - 1:
                columns += [lowers[image][:]]
            for h, column in enumerate(columns):
                nc.tensor.transpose(
                    out=spread[:, h * P : (h + 1) * P],
                    in_=column.to_broadcast([P, P]),
                    identity=ident[:],
                )
            spreads[image] = spread

        def exponentials(image):
            shift = small.tile([P, 1], F32, tag="shift")
            sources = slice(PIXELS, PIXELS + P) if image < IMAGES - 1 else slice(0, PIXELS)
            nc.vector.tensor_reduce(out=shift[:], in_=spreads[image][:, sources], axis=AXIS_X, op=ALU.min)
            numer = small.tile([P, PIXELS], F32, tag="numer")
            denom = small.tile([P, 1], F32, tag="denom")
            nc.scalar.activation(
                out=numer[:],
                in_=spreads[image][:, 0:PIXELS],
                func=ACT.Exp,
                bias=shift[:, 0:1],
                scale=-1.0,
                accum_out=denom[:],
            )
            numers[image] = numer
            denoms[image] = denom

        def multiply_on_vector(image, row):
            nc.vector.scalar_tensor_tensor(
                out=products[image][:, row, :],
                in0=x_sb[:, image, row, :],
                scalar=inverses[image][:, 0:1],
                in1=numers[image][:],
                op0=ALU.mult,
                op1=ALU.mult,
            )

        def gate_and_store(image):
            inverse = small.tile([P, 1], F32, tag="inverse")
            nc.vector.reciprocal(out=inverse[:], in_=denoms[image][:])
            inverses[image] = inverse
            product = results.tile([P, PACK, PIXELS], F32, tag="product")
            products[image] = product
            if image == IMAGES - 1:
                for row in range(PACK):
                    multiply_on_vector(image, row)
                    nc.sync.dma_start(out=out_view[image][:, row, :], in_=product[:, row, :])
                return
            if image == IMAGES - 2:
                return
            gate = small.tile([P, PIXELS], F32, tag="gate")
            nc.scalar.activation(out=gate[:], in_=numers[image][:], func=ACT.Copy, scale=inverse[:, 0:1])
            nc.gpsimd.tensor_tensor(
                out=product[:],
                in0=x_sb[:, image],
                in1=gate[:].unsqueeze(1).to_broadcast([P, PACK, PIXELS]),
                op=ALU.mult,
            )
            nc.sync.dma_start(out=out_view[image], in_=product[:])

        def multiply_second_last(first, count):
            image = IMAGES - 2
            for row in range(first, first + count):
                multiply_on_vector(image, row)
            rows = slice(first, first + count)
            nc.sync.dma_start(out=out_view[image][:, rows, :], in_=products[image][:, rows, :])

        def endings(n):
            if n == len(units):
                multiply_second_last(0, 3)
            if n == len(units) + EXP_LAG:
                multiply_second_last(3, 1)
            for image in range(IMAGES):
                last_unit = max(units.index((2 * image + h, pair)) for h in range(2) for pair in range(PAIRS))
                if 2 * image < EARLY_CHUNKS:
                    last_unit += EARLY_DELAY
                if n == last_unit:
                    add_up(image)
                if n == last_unit + SPREAD_LAG:
                    spread_out(image)
                if n == last_unit + EXP_LAG:
                    exponentials(image)
                if n == last_unit + GATE_LAG:
                    gate_and_store(image)

        wk_grouped = new_w_grouped()
        wq_grouped = new_w_grouped()
        warm_up(5)
        turn_half(wk_rows, wk_grouped, 0, on_vector=False)
        warm_up(1)
        turn_half(wk_rows, wk_grouped, 1, on_vector=False)
        warm_up(1)
        regroup_x(0, "vector")
        quantise_x(0)
        regroup_x(1, "vector")
        quantise_w_half(sides["k"], wk_grouped, 0)
        quantise_x(1)
        quantise_w_half(sides["k"], wk_grouped, 1)
        turn_half(wq_rows, wq_grouped, 0, on_vector=False)
        warm_up(1)
        project("k", 0, (0,))
        turn_half(wq_rows, wq_grouped, 1, on_vector=False)
        project("k", 0, (1, 2, 3))
        regroup_x(2, "vector")
        regroup_x(3, "vector")
        quantise_w_half(sides["q"], wq_grouped, 0)
        quantise_x(2)
        quantise_x(3)
        quantise_w_half(sides["q"], wq_grouped, 1)
        regroup_x(5, "vector")
        project("q", 0, (3,), on_vector=True)
        project("q", 0, range(3))
        regroup("k", 0, 0, "vector")
        regroup("k", 0, 1, "vector")
        project("k", 1, range(4))
        warm_up(2)
        quantise_half("k", 0, 0)
        quantise_half("k", 0, 1)
        regroup("q", 0, 0, "vector")
        regroup("q", 0, 1, "vector")
        regroup("k", 1, 0, "scalar")
        quantise_half("q", 0, 0)
        score_pass(0)
        score_pass(1)
        quantise_half("q", 0, 1)
        regroup("k", 1, 1, "gpsimd")
        regroup_x(4, "vector")

        before = {
            3: [lambda: quantise("k", 1), lambda: quantise_x(4), lambda: quantise_x(5), lambda: regroup("q", 1, 1, "gpsimd")],
            7: [lambda: quantise("q", 1)],
            14: [lambda: quantise("k", 2), lambda: regroup("q", 2, 1, "gpsimd")],
            17: [lambda: quantise_x(6), lambda: quantise_x(7)],
            22: [lambda: quantise("q", 2)],
            29: [lambda: quantise("k", 3), lambda: regroup("q", 3, 1, "gpsimd")],
            36: [lambda: quantise("q", 3)],
        }
        after = {
            0: [lambda: project("q", 1, range(4)), lambda: regroup("q", 1, 0, "scalar")],
            3: [lambda: project("k", 2, (0, 1))],
            4: [lambda: project("k", 2, (2, 3)), lambda: regroup("k", 2, 0, "scalar"), lambda: regroup_x(6, "scalar"), lambda: regroup_x(7, "scalar")],
            7: [lambda: regroup("k", 2, 1, "gpsimd")],
            9: [lambda: project("q", 2, (0, 1))],
            10: [lambda: project("q", 2, (2, 3)), lambda: regroup("q", 2, 0, "scalar")],
            17: [lambda: project("k", 3, (0, 1))],
            18: [lambda: project("k", 3, (2, 3)), lambda: regroup("k", 3, 0, "scalar")],
            22: [lambda: regroup("k", 3, 1, "gpsimd")],
            23: [lambda: project("q", 3, (0, 1))],
            24: [lambda: project("q", 3, (2, 3)), lambda: regroup("q", 3, 0, "scalar")],
        }
        issued = 2
        for n in range(len(units) + GATE_LAG + 1):
            for step in before.get(n, []):
                step()
            while issued < min(n + LEAD + 1, len(units)) and available(issued):
                score_pass(issued)
                issued += 1
            if n < len(units):
                take_maxima(n)
            for step in after.get(n, []):
                step()
            endings(n)
